import numpy as np
import ml_dtypes


def mxq(x, axis, fmt="e4m3"):
    dtype, down = {"e4m3": (ml_dtypes.float8_e4m3fn, 7), "e5m2": (ml_dtypes.float8_e5m2, 14)}[fmt]
    v = np.moveaxis(np.asarray(x, np.float32).astype(ml_dtypes.bfloat16).astype(np.float64), axis, -1)
    blocks = v.reshape(v.shape[:-1] + (-1, 32))
    amax = np.abs(blocks).max(-1, keepdims=True)
    byte = np.maximum(np.where(amax > 0, np.frexp(amax)[1] - 1 + 127, 0) - down, 1)
    scale = np.exp2(byte - 127.0)
    codes = (blocks / scale).astype(np.float32).astype(dtype).astype(np.float64)
    return np.moveaxis((codes * scale).reshape(v.shape), -1, axis)


WIDE = False


def mx_kscale(k):
    if not WIDE:
        return np.ones(k)
    levels = np.array([10, -10, 5, -5, 0])
    if k % 512:
        return np.exp2(np.random.permutation(np.resize(levels, k // 32))).repeat(32)
    a = np.empty((k // 512, 16))
    for p in range(k // 512):
        a[p, :8] = np.random.permutation(np.resize(levels, 8))
        for g in range(8):
            far = levels[np.abs(levels - a[p, g]) >= 10]
            a[p, g + 8] = far[np.random.randint(len(far))]
    return np.exp2(a.ravel()).repeat(32)


BF16 = ml_dtypes.bfloat16


def bf(x):
    return np.asarray(x, np.float32).astype(BF16)


def f64(x):
    return np.asarray(x).astype(np.float64)


B, G, M, S, H = 256, 10, 4, 512, 512
ALPHA = 1.1


def entmax(alpha, v):
    v = v - np.max(v, axis=-1, keepdims=True)
    e = np.exp(v)
    s = (np.sum(e ** alpha, axis=-1, keepdims=True) + 1e-5) ** (1.0 / alpha)
    return e / s


def layernorm(h, w, b):
    mu = np.mean(h, axis=-1, keepdims=True)
    var = np.mean((h - mu) ** 2, axis=-1, keepdims=True)
    return (h - mu) * (1.0 / np.sqrt(var + 1e-5)) * w + b


def sigmoid(v):
    return 1.0 / (1.0 + np.exp(-v))


def group_matmul(a, w):
    nb, ng, nm, ns = a.shape
    y = a.transpose(1, 0, 2, 3).reshape(ng, nb * nm, ns) @ w.transpose(0, 2, 1)
    return y.reshape(ng, nb, nm, w.shape[1]).transpose(1, 0, 2, 3)


def setup_inputs():
    k = mx_kscale(S)
    ws = 0.003 * S ** (1.0 / ALPHA - 0.5)
    return {"x": bf(np.random.standard_normal((B, G * S)) * np.tile(k, G)),
            "W_masks": bf(np.random.standard_normal((G, M, S))),
            "W1": bf((np.random.standard_normal((G, H, S)) + 0.3) * ws / k),
            "W2": bf((np.random.standard_normal((G, H, S)) + 0.3) * ws / k),
            "ln1_w": bf(1.0 + 0.2 * np.random.standard_normal((G, H))),
            "ln1_b": bf(0.2 * np.random.standard_normal((G, H))),
            "ln2_w": bf(1.0 + 0.2 * np.random.standard_normal((G, H))),
            "ln2_b": bf(0.2 * np.random.standard_normal((G, H)))}


def reference(x, W_masks, W1, W2, ln1_w, ln1_b, ln2_w, ln2_b):
    g, m, s = W_masks.shape
    b = x.shape[0]
    xg = f64(x).reshape(b, g, s)
    mask = entmax(ALPHA, f64(W_masks))
    weighted = xg[:, :, None, :] * mask[None]
    wq = mxq(weighted, 3, "e4m3")
    h1 = group_matmul(wq, mxq(f64(W1), 2, "e4m3"))
    h2 = group_matmul(wq, mxq(f64(W2), 2, "e4m3"))
    n1 = layernorm(h1, f64(ln1_w)[None, :, None, :], f64(ln1_b)[None, :, None, :])
    n2 = layernorm(h2, f64(ln2_w)[None, :, None, :], f64(ln2_b)[None, :, None, :])
    activated = np.maximum(sigmoid(n1) * n2, 0.0)
    group_out = np.sum(activated, axis=2)
    return group_out.reshape(b, g * group_out.shape[-1])

@@ -1,0 +1,358 @@
+from contextlib import ExitStack
+
+import concourse.mybir as mybir
+from concourse.masks import make_identity
+
+F32 = mybir.dt.float32
+BF16 = mybir.dt.bfloat16
+U32 = mybir.dt.uint32
+U8 = mybir.dt.uint8
+FP8X4 = mybir.dt.float8_e4m3fn_x4
+ALU = mybir.AluOpType
+ACT = mybir.ActivationFunctionType
+AX = mybir.AxisListType
+
+B, G, M, S, H = 256, 10, 4, 512, 512
+ALPHA = 1.1
+EPS = 1e-5
+P = 128
+FLOPS = 2 * 2 * B * G * M * S * H
+
+NSTEP = G * 2 * M
+NSS = G * 2
+GM = G * M
+V_TAKES_Z = 72
+V_TAKES_RELU = 80
+
+
+def tile_dynamicfeaturegroupinglayer_kernel(tc, x, W_masks, W1, W2, ln1_w, ln1_b, ln2_w, ln2_b, out):
+    nc = tc.nc
+    with ExitStack() as ctx:
+        ctx.enter_context(tc.manual_schedule())
+        const = ctx.enter_context(tc.tile_pool(name="const", bufs=1))
+        wrawp = ctx.enter_context(tc.tile_pool(name="wrawp", bufs=3))
+        prepp = ctx.enter_context(tc.tile_pool(name="prepp", bufs=2))
+        wtp = ctx.enter_context(tc.tile_pool(name="wtp", bufs=4))
+        small = ctx.enter_context(tc.tile_pool(name="small", bufs=4))
+        zp = ctx.enter_context(tc.tile_pool(name="zp", bufs=2))
+        ap3 = ctx.enter_context(tc.tile_pool(name="ap3", bufs=3))
+        outp = ctx.enter_context(tc.tile_pool(name="outp", bufs=2))
+        pa = ctx.enter_context(tc.psum_pool(name="pa", bufs=2))
+        pb = ctx.enter_context(tc.psum_pool(name="pb", bufs=2))
+        pz = ctx.enter_context(tc.psum_pool(name="pz", bufs=2))
+        pprep = ctx.enter_context(tc.psum_pool(name="pprep", bufs=1))
+        pfin = ctx.enter_context(tc.psum_pool(name="pfin", bufs=1))
+
+        wm = const.tile([P, S], BF16, name="wm")
+        nc.sync.dma_start(out=wm[0:GM, :], in_=W_masks.rearrange("g m s -> (g m) s"))
+        x_sb = const.tile([P, 2, G * S], BF16, name="x_sb")
+        for bh in range(2):
+            nc.sync.dma_start(out=x_sb[:, bh, 0:S], in_=x[bh * P:(bh + 1) * P, 0:S])
+
+        wraw = {}
+
+        def load_w(g):
+            t_ = wrawp.tile([P, 2, 4, S], BF16, name="wraw", tag="wraw")
+            nc.sync.dma_start(out=t_[:, 0], in_=W1[g].rearrange("(t p) s -> p t s", p=P))
+            nc.sync.dma_start(out=t_[:, 1], in_=W2[g].rearrange("(t p) s -> p t s", p=P))
+            wraw[g] = t_
+
+        load_w(0)
+        lnraw = const.tile([P, 2, P], BF16, name="lnraw")
+        nc.vector.memset(lnraw[:], 0.0)
+        nc.sync.dma_start(out=lnraw[0:GM, 0, :], in_=ln1_w.rearrange("g (t p) -> (g t) p", p=P))
+        nc.sync.dma_start(out=lnraw[GM:2 * GM, 0, :], in_=ln1_b.rearrange("g (t p) -> (g t) p", p=P))
+        nc.sync.dma_start(out=lnraw[0:GM, 1, :], in_=ln2_w.rearrange("g (t p) -> (g t) p", p=P))
+        nc.sync.dma_start(out=lnraw[GM:2 * GM, 1, :], in_=ln2_b.rearrange("g (t p) -> (g t) p", p=P))
+        for bh in range(2):
+            nc.sync.dma_start(out=x_sb[:, bh, S:G * S], in_=x[bh * P:(bh + 1) * P, S:G * S])
+        load_w(1)
+
+        ident = const.tile([P, P], F32, name="ident")
+        make_identity(nc, ident[:])
+        one = const.tile([P, 1], F32, name="one")
+        nc.vector.memset(one[:], 1.0)
+        warm = const.tile([P, 1], F32, name="warm")
+        nc.scalar.activation(out=warm[:], in_=one[:], func=ACT.Exp)
+        cexp = const.tile([P, 2], F32, name="cexp")
+        nc.vector.memset(cexp[:], -0.5)
+        cal = const.tile([P, 1], F32, name="cal")
+        nc.vector.tensor_scalar(out=cal[:], in0=one[:], scalar1=-1.0 / ALPHA, scalar2=None, op0=ALU.mult)
+        mask_sb = const.tile([P, S], F32, name="mask_sb")
+        nc.vector.memset(mask_sb[:], 0.0)
+
+        mx_ = const.tile([P, 1], F32, name="mx_")
+        nc.vector.reduce_max(out=mx_[0:GM, :], in_=wm[0:GM, :], axis=AX.X)
+        nmx = const.tile([P, 1], F32, name="nmx")
+        nc.vector.tensor_scalar(out=nmx[0:GM, :], in0=mx_[0:GM, :], scalar1=-1.0, scalar2=None, op0=ALU.mult)
+        nmxa = const.tile([P, 1], F32, name="nmxa")
+        nc.vector.tensor_scalar(out=nmxa[0:GM, :], in0=mx_[0:GM, :], scalar1=-ALPHA, scalar2=None, op0=ALU.mult)
+        ea_sb = const.tile([P, S], F32, name="ea_sb")
+        sa = const.tile([P, 1], F32, name="sa")
+        nc.scalar.activation(out=ea_sb[0:GM, :], in_=wm[0:GM, :], func=ACT.Exp, bias=nmxa[0:GM, :], scale=ALPHA,
+                             accum_out=sa[0:GM, :])
+        e_sb = const.tile([P, S], F32, name="e_sb")
+        nc.scalar.activation(out=e_sb[0:GM, :], in_=wm[0:GM, :], func=ACT.Exp, bias=nmx[0:GM, :], scale=1.0)
+        sae = const.tile([P, 1], F32, name="sae")
+        nc.vector.tensor_scalar(out=sae[0:GM, :], in0=sa[0:GM, :], scalar1=EPS, scalar2=None, op0=ALU.add)
+        msc = const.tile([P, 1], F32, name="msc")
+        nc.gpsimd.tensor_tensor(out=msc[0:GM, :], in0=sae[0:GM, :], in1=cal[0:GM, :], op=ALU.pow)
+        nc.vector.tensor_scalar(out=mask_sb[0:GM, :], in0=e_sb[0:GM, :], scalar1=msc[0:GM, :], scalar2=None,
+                                op0=ALU.mult)
+        lnf = const.tile([P, 2, P], F32, name="lnf")
+        nc.vector.tensor_copy(out=lnf[:], in_=lnraw[:])
+
+        gw, wc, ws, xc, xs, xbank, wt, fillb = {}, {}, {}, {}, {}, {}, {}, {}
+
+        def wfill_t(g, f, pool, tag):
+            w, jh = f // 2, f % 2
+            bank = pool.tile([P, 2, 256], F32, name="wbank", tag=tag)
+            for u in range(2):
+                for jl in range(2):
+                    src = wraw[g][:, w, 2 * jh + jl, :].bitcast(F32)
+                    nc.tensor.transpose(bank[:, u, jl * P:(jl + 1) * P], src[:, u:256:2], ident[:])
+            fillb[(g, f)] = bank
+
+        def wfill_copy(g, f, on_scalar):
+            w, jh = f // 2, f % 2
+            if jh == 0:
+                gw[(g, w)] = prepp.tile([P, 4 * H], BF16, name="gw", tag="gw", align_bytes=64)
+            dst = gw[(g, w)][:].bitcast(F32).rearrange("p (j u) -> p j u", u=2)
+            src = fillb[(g, f)][:].rearrange("p u j -> p j u")
+            if on_scalar:
+                nc.scalar.copy(out=dst[:, jh * 256:(jh + 1) * 256, :], in_=src)
+            else:
+                nc.vector.tensor_copy(out=dst[:, jh * 256:(jh + 1) * 256, :], in_=src)
+
+        def quant_w(g, w):
+            if w == 0:
+                wc[g] = prepp.tile([P, 2, H], U32, name="wc", tag="wc", align_bytes=64)
+                ws[g] = prepp.tile([P, 2, H], U8, name="ws", tag="ws", align_bytes=64)
+            nc.vector.quantize_mx(out=wc[g][:, w, :].bitcast(FP8X4), scales=ws[g][:, w, :], in_=gw[(g, w)][:])
+
+        def x_t(g):
+            bank = pprep.tile([P, 2, 256], F32, name="xbank", tag="prep")
+            for u in range(2):
+                for bh in range(2):
+                    src = x_sb[:, bh, :].bitcast(F32)
+                    nc.tensor.transpose(bank[:, u, bh * P:(bh + 1) * P],
+                                        src[:, 256 * g + u:256 * (g + 1):2], ident[:])
+            xbank[g] = bank
+
+        def weighted(g, m):
+            t_ = wtp.tile([P, 4 * B], BF16, name="wt", tag="wt", align_bytes=64)
+            in0 = xbank[g][:].rearrange("p u b -> p (u b)").bitcast(BF16).rearrange("p (u b e) -> p b u e", u=2, e=2)
+            in1 = maskT[:, g * M + m, :].rearrange("p (u e) -> p u e", u=2).unsqueeze(1).to_broadcast([P, B, 2, 2])
+            nc.vector.tensor_tensor(out=t_[:].rearrange("p (b u e) -> p b u e", u=2, e=2), in0=in0, in1=in1,
+                                    op=ALU.mult)
+            wt[(g, m)] = t_
+
+        def quant_x(g, m):
+            if m == 0:
+                xc[g] = prepp.tile([P, M, B], U32, name="xc", tag="xc", align_bytes=64)
+                xs[g] = prepp.tile([P, M, B], U8, name="xs", tag="xs", align_bytes=64)
+            nc.vector.quantize_mx(out=xc[g][:, m, :].bitcast(FP8X4), scales=xs[g][:, m, :], in_=wt[(g, m)][:])
+
+        sts, mvt, vet, nmt, rst, nbt = {}, {}, {}, {}, {}, {}
+        ha, hb, zt, zbank, sig, r2, prod, finb = {}, {}, {}, {}, {}, {}, {}, {}
+
+        def mx(t, second):
+            g, bh, m = t // 8, (t % 8) // 4, t % 4
+            cols = slice(bh * P, (bh + 1) * P)
+            pair = []
+            for w in range(2):
+                if second:
+                    bank = pb.tile([P, H], F32, name="hb", tag="hb")
+                else:
+                    bank = pa.tile([P, H], F32, name="ha", tag="ha")
+                nc.tensor.matmul_mx(out=bank[:], lhsT=xc[g][:, m, cols].bitcast(FP8X4), lhsT_scale=xs[g][:, m, cols],
+                                    rhs=wc[g][:, w, :].bitcast(FP8X4), rhs_scale=ws[g][:, w, :],
+                                    start=True, stop=True)
+                pair.append(bank)
+            if second:
+                hb[t] = pair
+            else:
+                ha[t] = pair
+
+        def bn(t):
+            sts[t] = small.tile([P, 2, 6], F32, name="st", tag="st")
+            for w in range(2):
+                nc.vector.bn_stats(out=sts[t][:, w, :], in_=ha[t][w][:])
+
+        def ag(t):
+            mvt[t] = small.tile([P, 2, 2], F32, name="mv", tag="mv")
+            for w in range(2):
+                nc.vector.bn_aggr(out=mvt[t][:, w, :], in_=sts[t][:, w, :])
+
+        def vn(t):
+            vet[t] = small.tile([P, 2], F32, name="ve", tag="ve")
+            nc.vector.tensor_scalar(out=vet[t][:], in0=mvt[t][:, :, 1], scalar1=EPS, scalar2=None, op0=ALU.add)
+            nmt[t] = small.tile([P, 2], F32, name="nm", tag="nm")
+            nc.vector.tensor_scalar(out=nmt[t][:], in0=mvt[t][:, :, 0], scalar1=-1.0, scalar2=None, op0=ALU.mult)
+
+        def ch_rs(t):
+            rst[t] = small.tile([P, 2], F32, name="rs", tag="rs")
+            nc.gpsimd.tensor_tensor(out=rst[t][:], in0=vet[t][:], in1=cexp[:], op=ALU.pow)
+
+        def ch_nb(t):
+            nbt[t] = small.tile([P, 2], F32, name="nb", tag="nb")
+            nc.gpsimd.tensor_tensor(out=nbt[t][:], in0=nmt[t][:], in1=rst[t][:], op=ALU.mult)
+
+        def z_dst(t, w):
+            ss, m = t // 4, t % 4
+            if ss not in zt:
+                zt[ss] = zp.tile([P, 2, M, H], F32, name="z", tag="z")
+            return zt[ss][:, w, m, :]
+
+        def z_scalar(t, w):
+            nc.scalar.activation(out=z_dst(t, w), in_=hb[t][w][:], func=ACT.Identity,
+                                 bias=nbt[t][:, w:w + 1], scale=rst[t][:, w:w + 1])
+
+        def z_vector(t, w):
+            nc.vector.tensor_scalar(out=z_dst(t, w), in0=hb[t][w][:], scalar1=mvt[t][:, w, 0:1],
+                                    scalar2=rst[t][:, w:w + 1], op0=ALU.subtract, op1=ALU.mult)
+
+        def tr(ss, k):
+            jt, w = k // 2, k % 2
+            bank = pz.tile([P, M, P], F32, name="zT", tag="zT")
+            for m in range(M):
+                nc.tensor.transpose(bank[:, m, :], zt[ss][:, w, m, jt * P:(jt + 1) * P], ident[:])
+            zbank[(ss, k)] = bank
+
+        def act_sig(ss, jt):
+            c = (ss // 2) * 4 + jt
+            sig[(ss, jt)] = ap3.tile([P, M * P], F32, name="sig", tag="sig")
+            nc.scalar.activation(out=sig[(ss, jt)][:], in_=zbank[(ss, 2 * jt)][:].rearrange("p m b -> p (m b)"),
+                                 func=ACT.Sigmoid, bias=lnT[:, 0, GM + c:GM + c + 1], scale=lnT[:, 0, c:c + 1])
+
+        def act_relu(ss, jt, on_vector):
+            c = (ss // 2) * 4 + jt
+            r2[(ss, jt)] = ap3.tile([P, M * P], F32, name="r2", tag="r2")
+            src = zbank[(ss, 2 * jt + 1)][:].rearrange("p m b -> p (m b)")
+            if on_vector:
+                nc.vector.tensor_scalar(out=r2[(ss, jt)][:], in0=src, scalar1=lnT[:, 1, c:c + 1],
+                                        scalar2=lnT[:, 1, GM + c:GM + c + 1], op0=ALU.mult, op1=ALU.add)
+            else:
+                nc.scalar.activation(out=r2[(ss, jt)][:], in_=src, func=ACT.Relu,
+                                     bias=lnT[:, 1, GM + c:GM + c + 1], scale=lnT[:, 1, c:c + 1])
+
+        def mul(ss, jt, on_vector):
+            prod[(ss, jt)] = ap3.tile([P, M, P], F32, name="prod", tag="prod")
+            dst = prod[(ss, jt)][:].rearrange("p m b -> p (m b)")
+            if on_vector:
+                nc.vector.scalar_tensor_tensor(out=dst, in0=r2[(ss, jt)][:], scalar=0.0, in1=sig[(ss, jt)][:],
+                                               op0=ALU.max, op1=ALU.mult)
+            else:
+                nc.gpsimd.tensor_tensor(out=dst, in0=sig[(ss, jt)][:], in1=r2[(ss, jt)][:], op=ALU.mult)
+
+        def acc(ss, jt):
+            if jt == 0:
+                finb[ss] = pfin.tile([P, H], F32, name="fin", tag="fin")
+            for m in range(M):
+                nc.tensor.matmul(finb[ss][:, jt * P:(jt + 1) * P], lhsT=prod[(ss, jt)][:, m, :], rhs=ident[:],
+                                 is_transpose=True, start=(m == 0), stop=(m == M - 1))
+
+        def fin(ss):
+            g, bh = ss // 2, ss % 2
+            ot = outp.tile([P, H], F32, name="ot", tag="ot")
+            nc.scalar.copy(out=ot[:], in_=finb[ss][:])
+            nc.sync.dma_start(out=out[bh * P:(bh + 1) * P, g * H:(g + 1) * H], in_=ot[:])
+
+        x_t(0)
+        for f in range(4):
+            if f < 2:
+                wfill_t(0, f, pa, "ha")
+            else:
+                wfill_t(0, f, pb, "hb")
+            wfill_copy(0, f, True)
+        mps = pz.tile([P, 4, P], F32, name="mps", tag="zT")
+        for u in range(2):
+            for e in range(2):
+                nc.tensor.transpose(mps[:, 2 * u + e, :], mask_sb[:, 2 * u + e:S:4], ident[:])
+        lps = pz.tile([P, 2, P], F32, name="lps", tag="zT")
+        for a in range(2):
+            nc.tensor.transpose(lps[:, a, :], lnf[:, a, :], ident[:])
+        quant_w(0, 0)
+        maskT = const.tile([P, GM, 4], F32, name="maskT")
+        nc.vector.tensor_copy(out=maskT[:], in_=mps[:, :, 0:GM].rearrange("p t c -> p c t"))
+        weighted(0, 0)
+        quant_w(0, 1)
+        quant_x(0, 0)
+        mx(0, False)
+        weighted(0, 1)
+        lnT = const.tile([P, 2, P], F32, name="lnT")
+        nc.vector.tensor_copy(out=lnT[:], in_=lps[:])
+        quant_x(0, 1)
+        weighted(0, 2)
+        weighted(0, 3)
+        quant_x(0, 2)
+        x_t(1)
+        quant_x(0, 3)
+        weighted(1, 0)
+
+        def prep_v1(g, k, t):
+            if 0 <= k < 4:
+                weighted(g, k)
+            elif 4 <= k < 8:
+                wfill_copy(g, k - 4, t < 8 or k == 6)
+
+        def prep_v2(g, k, t):
+            if k in (4, 5):
+                quant_x(g, 2 * k - 8)
+                quant_x(g, 2 * k - 7)
+            elif k in (6, 7):
+                quant_w(g, k - 6)
+
+        def prep_pe(g, k, t):
+            if k == -1:
+                x_t(g)
+            elif 3 <= k < 7:
+                wfill_t(g, k - 3, pprep, "prep")
+
+        def prep(t, part):
+            for gq in range(1, G):
+                k = t - (8 * (gq - 1) - 1)
+                if -1 <= k <= 7:
+                    part(gq, k, t)
+
+        for t in range(NSTEP + 8):
+            tb = t - 2
+            ta = tb - 4
+            tm = ta - 1
+            tf = tm - 1
+            if t % 8 == 0 and t // 8 + 2 < G:
+                load_w(t // 8 + 2)
+            if 0 <= tb < NSTEP:
+                mx(tb, True)
+            if t < NSTEP:
+                bn(t)
+            prep(t, prep_v1)
+            if 0 <= t - 1 < NSTEP:
+                vn(t - 1)
+                ch_rs(t - 1)
+            prep(t, prep_v2)
+            if 0 <= tb < NSTEP and t >= V_TAKES_Z:
+                z_vector(tb, 1)
+            if t < NSTEP:
+                ag(t)
+            if t + 1 < NSTEP:
+                mx(t + 1, False)
+            if 0 <= ta < NSTEP:
+                tr(ta // 4, 2 * (ta % 4))
+                tr(ta // 4, 2 * (ta % 4) + 1)
+            if 0 <= tm < NSTEP:
+                mul(tm // 4, tm % 4, t - 1 >= V_TAKES_RELU)
+            if 0 <= t - 1 < NSTEP:
+                ch_nb(t - 1)
+            if 0 <= tb < NSTEP:
+                z_scalar(tb, 0)
+                if t < V_TAKES_Z:
+                    z_scalar(tb, 1)
+            if 0 <= ta < NSTEP:
+                act_sig(ta // 4, ta % 4)
+                act_relu(ta // 4, ta % 4, t >= V_TAKES_RELU)
+            if 0 <= tf < NSTEP:
+                acc(tf // 4, tf % 4)
+                if tf % 4 == 3:
+                    fin(tf // 4)
+            prep(t, prep_pe)

@@ -21,8 +21,9 @@ FLOPS = 2 * 2 * B * G * M * S * H
 NSTEP = G * 2 * M
 NSS = G * 2
 GM = G * M
-V_TAKES_Z = 72
-V_TAKES_RELU = 80
+V_TAKES_Z = 8 * (G - 1)
+V_TAKES_RELU = NSTEP
+NST = 4
 
 
 def tile_dynamicfeaturegroupinglayer_kernel(tc, x, W_masks, W1, W2, ln1_w, ln1_b, ln2_w, ln2_b, out):
@@ -37,8 +38,7 @@ def tile_dynamicfeaturegroupinglayer_kernel(tc, x, W_masks, W1, W2, ln1_w, ln1_b
         zp = ctx.enter_context(tc.tile_pool(name="zp", bufs=2))
         ap3 = ctx.enter_context(tc.tile_pool(name="ap3", bufs=3))
         outp = ctx.enter_context(tc.tile_pool(name="outp", bufs=2))
-        pa = ctx.enter_context(tc.psum_pool(name="pa", bufs=2))
-        pb = ctx.enter_context(tc.psum_pool(name="pb", bufs=2))
+        ph = ctx.enter_context(tc.psum_pool(name="ph", bufs=4))
         pz = ctx.enter_context(tc.psum_pool(name="pz", bufs=2))
         pprep = ctx.enter_context(tc.psum_pool(name="pprep", bufs=1))
         pfin = ctx.enter_context(tc.psum_pool(name="pfin", bufs=1))
@@ -58,6 +58,9 @@ def tile_dynamicfeaturegroupinglayer_kernel(tc, x, W_masks, W1, W2, ln1_w, ln1_b
             wraw[g] = t_
 
         load_w(0)
+        for bh in range(2):
+            nc.sync.dma_start(out=x_sb[:, bh, S:2 * S], in_=x[bh * P:(bh + 1) * P, S:2 * S])
+        load_w(1)
         lnraw = const.tile([P, 2, P], BF16, name="lnraw")
         nc.vector.memset(lnraw[:], 0.0)
         nc.sync.dma_start(out=lnraw[0:GM, 0, :], in_=ln1_w.rearrange("g (t p) -> (g t) p", p=P))
@@ -65,8 +68,7 @@ def tile_dynamicfeaturegroupinglayer_kernel(tc, x, W_masks, W1, W2, ln1_w, ln1_b
         nc.sync.dma_start(out=lnraw[0:GM, 1, :], in_=ln2_w.rearrange("g (t p) -> (g t) p", p=P))
         nc.sync.dma_start(out=lnraw[GM:2 * GM, 1, :], in_=ln2_b.rearrange("g (t p) -> (g t) p", p=P))
         for bh in range(2):
-            nc.sync.dma_start(out=x_sb[:, bh, S:G * S], in_=x[bh * P:(bh + 1) * P, S:G * S])
-        load_w(1)
+            nc.sync.dma_start(out=x_sb[:, bh, 2 * S:G * S], in_=x[bh * P:(bh + 1) * P, 2 * S:G * S])
 
         ident = const.tile([P, P], F32, name="ident")
         make_identity(nc, ident[:])
@@ -76,8 +78,18 @@ def tile_dynamicfeaturegroupinglayer_kernel(tc, x, W_masks, W1, W2, ln1_w, ln1_b
         nc.scalar.activation(out=warm[:], in_=one[:], func=ACT.Exp)
         cexp = const.tile([P, 2], F32, name="cexp")
         nc.vector.memset(cexp[:], -0.5)
+        cneg = const.tile([P, 2], F32, name="cneg")
+        nc.vector.memset(cneg[:], -1.0)
         cal = const.tile([P, 1], F32, name="cal")
         nc.vector.tensor_scalar(out=cal[:], in0=one[:], scalar1=-1.0 / ALPHA, scalar2=None, op0=ALU.mult)
+        ones = const.tile([P, 2], F32, name="ones")
+        nc.vector.memset(ones[:], 1.0)
+        stt = []
+        for i in range(NST):
+            st = const.tile([P, 2, 9], F32, name="st%d" % i)
+            nc.vector.memset(st[:], 0.0)
+            nc.vector.tensor_scalar(out=st[:, :, 8], in0=ones[:], scalar1=H * EPS, scalar2=None, op0=ALU.mult)
+            stt.append(st)
         mask_sb = const.tile([P, S], F32, name="mask_sb")
         nc.vector.memset(mask_sb[:], 0.0)
 
@@ -130,8 +142,8 @@ def tile_dynamicfeaturegroupinglayer_kernel(tc, x, W_masks, W1, W2, ln1_w, ln1_b
                 ws[g] = prepp.tile([P, 2, H], U8, name="ws", tag="ws", align_bytes=64)
             nc.vector.quantize_mx(out=wc[g][:, w, :].bitcast(FP8X4), scales=ws[g][:, w, :], in_=gw[(g, w)][:])
 
-        def x_t(g):
-            bank = pprep.tile([P, 2, 256], F32, name="xbank", tag="prep")
+        def x_t(g, pool, tag):
+            bank = pool.tile([P, 2, 256], F32, name="xbank", tag=tag)
             for u in range(2):
                 for bh in range(2):
                     src = x_sb[:, bh, :].bitcast(F32)
@@ -153,50 +165,35 @@ def tile_dynamicfeaturegroupinglayer_kernel(tc, x, W_masks, W1, W2, ln1_w, ln1_b
                 xs[g] = prepp.tile([P, M, B], U8, name="xs", tag="xs", align_bytes=64)
             nc.vector.quantize_mx(out=xc[g][:, m, :].bitcast(FP8X4), scales=xs[g][:, m, :], in_=wt[(g, m)][:])
 
-        sts, mvt, vet, nmt, rst, nbt = {}, {}, {}, {}, {}, {}
-        ha, hb, zt, zbank, sig, r2, prod, finb = {}, {}, {}, {}, {}, {}, {}, {}
+        mvt, rst, nrt, nbt = {}, {}, {}, {}
+        hbank, zt, zbank, sig, r2, prod, finb = {}, {}, {}, {}, {}, {}, {}
 
-        def mx(t, second):
+        def mx(t):
             g, bh, m = t // 8, (t % 8) // 4, t % 4
             cols = slice(bh * P, (bh + 1) * P)
-            pair = []
             for w in range(2):
-                if second:
-                    bank = pb.tile([P, H], F32, name="hb", tag="hb")
-                else:
-                    bank = pa.tile([P, H], F32, name="ha", tag="ha")
+                bank = ph.tile([P, H], F32, name="h", tag="h")
                 nc.tensor.matmul_mx(out=bank[:], lhsT=xc[g][:, m, cols].bitcast(FP8X4), lhsT_scale=xs[g][:, m, cols],
                                     rhs=wc[g][:, w, :].bitcast(FP8X4), rhs_scale=ws[g][:, w, :],
                                     start=True, stop=True)
-                pair.append(bank)
-            if second:
-                hb[t] = pair
-            else:
-                ha[t] = pair
+                hbank[(t, w)] = bank
 
         def bn(t):
-            sts[t] = small.tile([P, 2, 6], F32, name="st", tag="st")
             for w in range(2):
-                nc.vector.bn_stats(out=sts[t][:, w, :], in_=ha[t][w][:])
+                nc.vector.bn_stats(out=stt[t % NST][:, w, 0:6], in_=hbank[(t, w)][:])
 
         def ag(t):
             mvt[t] = small.tile([P, 2, 2], F32, name="mv", tag="mv")
             for w in range(2):
-                nc.vector.bn_aggr(out=mvt[t][:, w, :], in_=sts[t][:, w, :])
+                nc.vector.bn_aggr(out=mvt[t][:, w, :], in_=stt[t % NST][:, w, :])
 
-        def vn(t):
-            vet[t] = small.tile([P, 2], F32, name="ve", tag="ve")
-            nc.vector.tensor_scalar(out=vet[t][:], in0=mvt[t][:, :, 1], scalar1=EPS, scalar2=None, op0=ALU.add)
-            nmt[t] = small.tile([P, 2], F32, name="nm", tag="nm")
-            nc.vector.tensor_scalar(out=nmt[t][:], in0=mvt[t][:, :, 0], scalar1=-1.0, scalar2=None, op0=ALU.mult)
-
-        def ch_rs(t):
+        def chain(t):
             rst[t] = small.tile([P, 2], F32, name="rs", tag="rs")
-            nc.gpsimd.tensor_tensor(out=rst[t][:], in0=vet[t][:], in1=cexp[:], op=ALU.pow)
-
-        def ch_nb(t):
+            nc.gpsimd.tensor_tensor(out=rst[t][:], in0=mvt[t][:, :, 1], in1=cexp[:], op=ALU.pow)
+            nrt[t] = small.tile([P, 2], F32, name="nr", tag="nr")
+            nc.gpsimd.tensor_tensor(out=nrt[t][:], in0=rst[t][:], in1=cneg[:], op=ALU.mult)
             nbt[t] = small.tile([P, 2], F32, name="nb", tag="nb")
-            nc.gpsimd.tensor_tensor(out=nbt[t][:], in0=nmt[t][:], in1=rst[t][:], op=ALU.mult)
+            nc.gpsimd.tensor_tensor(out=nbt[t][:], in0=mvt[t][:, :, 0], in1=rst[t][:], op=ALU.mult)
 
         def z_dst(t, w):
             ss, m = t // 4, t % 4
@@ -205,12 +202,12 @@ def tile_dynamicfeaturegroupinglayer_kernel(tc, x, W_masks, W1, W2, ln1_w, ln1_b
             return zt[ss][:, w, m, :]
 
         def z_scalar(t, w):
-            nc.scalar.activation(out=z_dst(t, w), in_=hb[t][w][:], func=ACT.Identity,
-                                 bias=nbt[t][:, w:w + 1], scale=rst[t][:, w:w + 1])
+            nc.scalar.activation(out=z_dst(t, w), in_=hbank[(t, w)][:], func=ACT.Identity,
+                                 bias=nbt[t][:, w:w + 1], scale=nrt[t][:, w:w + 1])
 
         def z_vector(t, w):
-            nc.vector.tensor_scalar(out=z_dst(t, w), in0=hb[t][w][:], scalar1=mvt[t][:, w, 0:1],
-                                    scalar2=rst[t][:, w:w + 1], op0=ALU.subtract, op1=ALU.mult)
+            nc.vector.tensor_scalar(out=z_dst(t, w), in0=hbank[(t, w)][:], scalar1=mvt[t][:, w, 0:1],
+                                    scalar2=nrt[t][:, w:w + 1], op0=ALU.subtract, op1=ALU.mult)
 
         def tr(ss, k):
             jt, w = k // 2, k % 2
@@ -258,18 +255,14 @@ def tile_dynamicfeaturegroupinglayer_kernel(tc, x, W_masks, W1, W2, ln1_w, ln1_b
             nc.scalar.copy(out=ot[:], in_=finb[ss][:])
             nc.sync.dma_start(out=out[bh * P:(bh + 1) * P, g * H:(g + 1) * H], in_=ot[:])
 
-        x_t(0)
-        for f in range(4):
-            if f < 2:
-                wfill_t(0, f, pa, "ha")
-            else:
-                wfill_t(0, f, pb, "hb")
-            wfill_copy(0, f, True)
         mps = pz.tile([P, 4, P], F32, name="mps", tag="zT")
-        for u in range(2):
-            for e in range(2):
-                nc.tensor.transpose(mps[:, 2 * u + e, :], mask_sb[:, 2 * u + e:S:4], ident[:])
-        lps = pz.tile([P, 2, P], F32, name="lps", tag="zT")
+        x_t(0, pz, "zT")
+        for f in range(4):
+            wfill_t(0, f, ph, "h")
+            wfill_copy(0, f, True)
+        for q in range(4):
+            nc.tensor.transpose(mps[:, q, :], mask_sb[:, q:S:4], ident[:])
+        lps = pfin.tile([P, 2, P], F32, name="lps", tag="fin")
         for a in range(2):
             nc.tensor.transpose(lps[:, a, :], lnf[:, a, :], ident[:])
         quant_w(0, 0)
@@ -278,76 +271,86 @@ def tile_dynamicfeaturegroupinglayer_kernel(tc, x, W_masks, W1, W2, ln1_w, ln1_b
         weighted(0, 0)
         quant_w(0, 1)
         quant_x(0, 0)
-        mx(0, False)
-        weighted(0, 1)
+        mx(0)
+        x_t(1, pz, "zT")
+        wfill_t(1, 0, pprep, "prep")
         lnT = const.tile([P, 2, P], F32, name="lnT")
-        nc.vector.tensor_copy(out=lnT[:], in_=lps[:])
+        weighted(0, 1)
+        nc.vector.tensor_scalar(out=lnT[:, :, 0:GM], in0=lps[:, :, 0:GM], scalar1=-1.0, scalar2=None, op0=ALU.mult)
+        nc.vector.tensor_copy(out=lnT[:, :, GM:2 * GM], in_=lps[:, :, GM:2 * GM])
         quant_x(0, 1)
-        weighted(0, 2)
-        weighted(0, 3)
-        quant_x(0, 2)
-        x_t(1)
-        quant_x(0, 3)
-        weighted(1, 0)
 
-        def prep_v1(g, k, t):
-            if 0 <= k < 4:
+        def prep_v(t):
+            if t < 2:
+                weighted(0, t + 2)
+                if t == 1:
+                    weighted(1, 0)
+                quant_x(0, t + 2)
+            elif t < 5:
+                weighted(1, t - 1)
+                quant_x(1, t - 2)
+            elif t == 5:
+                quant_x(1, 3)
+                quant_w(1, 0)
+            elif t == 6:
+                quant_w(1, 1)
+            g, k = (t + 1) // 8 + 1, (t + 1) % 8
+            if g < 2 or g >= G:
+                return
+            if k < 4:
                 weighted(g, k)
-            elif 4 <= k < 8:
-                wfill_copy(g, k - 4, t < 8 or k == 6)
+            else:
+                wfill_copy(g, k - 4, False)
+                if k == 4:
+                    quant_x(g, 0)
+                    quant_x(g, 1)
+                elif k == 5:
+                    quant_x(g, 2)
+                elif k == 6:
+                    quant_w(g, 0)
+                else:
+                    quant_x(g, 3)
+                    quant_w(g, 1)
 
-        def prep_v2(g, k, t):
-            if k in (4, 5):
-                quant_x(g, 2 * k - 8)
-                quant_x(g, 2 * k - 7)
-            elif k in (6, 7):
-                quant_w(g, k - 6)
+        def prep_s(t):
+            if t < 4:
+                wfill_copy(1, t, True)
 
-        def prep_pe(g, k, t):
-            if k == -1:
-                x_t(g)
-            elif 3 <= k < 7:
-                wfill_t(g, k - 3, pprep, "prep")
+        def prep_pe(t):
+            if t < 3:
+                wfill_t(1, t + 1, pprep, "prep")
+            g, k = (t + 2) // 8 + 1, (t + 2) % 8
+            if g < 2 or g >= G:
+                return
+            if k == 0:
+                x_t(g, pprep, "prep")
+            elif k >= 4:
+                wfill_t(g, k - 4, pprep, "prep")
 
-        def prep(t, part):
-            for gq in range(1, G):
-                k = t - (8 * (gq - 1) - 1)
-                if -1 <= k <= 7:
-                    part(gq, k, t)
-
-        for t in range(NSTEP + 8):
-            tb = t - 2
-            ta = tb - 4
+        for t in range(NSTEP + 7):
+            tz = t - 1
+            ta = tz - 4
             tm = ta - 1
             tf = tm - 1
             if t % 8 == 0 and t // 8 + 2 < G:
                 load_w(t // 8 + 2)
-            if 0 <= tb < NSTEP:
-                mx(tb, True)
             if t < NSTEP:
                 bn(t)
-            prep(t, prep_v1)
-            if 0 <= t - 1 < NSTEP:
-                vn(t - 1)
-                ch_rs(t - 1)
-            prep(t, prep_v2)
-            if 0 <= tb < NSTEP and t >= V_TAKES_Z:
-                z_vector(tb, 1)
-            if t < NSTEP:
                 ag(t)
-            if t + 1 < NSTEP:
-                mx(t + 1, False)
+                prep_v(t)
             if 0 <= ta < NSTEP:
                 tr(ta // 4, 2 * (ta % 4))
                 tr(ta // 4, 2 * (ta % 4) + 1)
+            if 0 <= tz < NSTEP:
+                z_scalar(tz, 0)
+                if t < V_TAKES_Z:
+                    z_scalar(tz, 1)
+                else:
+                    z_vector(tz, 1)
             if 0 <= tm < NSTEP:
                 mul(tm // 4, tm % 4, t - 1 >= V_TAKES_RELU)
-            if 0 <= t - 1 < NSTEP:
-                ch_nb(t - 1)
-            if 0 <= tb < NSTEP:
-                z_scalar(tb, 0)
-                if t < V_TAKES_Z:
-                    z_scalar(tb, 1)
+            if t < NSTEP:
+                chain(t)
             if 0 <= ta < NSTEP:
                 act_sig(ta // 4, ta % 4)
                 act_relu(ta // 4, ta % 4, t >= V_TAKES_RELU)
@@ -355,4 +358,8 @@ def tile_dynamicfeaturegroupinglayer_kernel(tc, x, W_masks, W1, W2, ln1_w, ln1_b
                 acc(tf // 4, tf % 4)
                 if tf % 4 == 3:
                     fin(tf // 4)
-            prep(t, prep_pe)
+            prep_s(t)
+            if t + 1 < NSTEP:
+                mx(t + 1)
+            if t < NSTEP:
+                prep_pe(t)

@@ -23,7 +23,7 @@ NSS = G * 2
 GM = G * M
 V_TAKES_Z = 8 * (G - 1)
 V_TAKES_RELU = NSTEP
-NST = 4
+NST = 2
 
 
 def tile_dynamicfeaturegroupinglayer_kernel(tc, x, W_masks, W1, W2, ln1_w, ln1_b, ln2_w, ln2_b, out):
@@ -38,7 +38,8 @@ def tile_dynamicfeaturegroupinglayer_kernel(tc, x, W_masks, W1, W2, ln1_w, ln1_b
         zp = ctx.enter_context(tc.tile_pool(name="zp", bufs=2))
         ap3 = ctx.enter_context(tc.tile_pool(name="ap3", bufs=3))
         outp = ctx.enter_context(tc.tile_pool(name="outp", bufs=2))
-        ph = ctx.enter_context(tc.psum_pool(name="ph", bufs=4))
+        ps = ctx.enter_context(tc.psum_pool(name="ps", bufs=2))
+        ph = ctx.enter_context(tc.psum_pool(name="ph", bufs=2))
         pz = ctx.enter_context(tc.psum_pool(name="pz", bufs=2))
         pprep = ctx.enter_context(tc.psum_pool(name="pprep", bufs=1))
         pfin = ctx.enter_context(tc.psum_pool(name="pfin", bufs=1))
@@ -76,17 +77,17 @@ def tile_dynamicfeaturegroupinglayer_kernel(tc, x, W_masks, W1, W2, ln1_w, ln1_b
         nc.vector.memset(one[:], 1.0)
         warm = const.tile([P, 1], F32, name="warm")
         nc.scalar.activation(out=warm[:], in_=one[:], func=ACT.Exp)
-        cexp = const.tile([P, 2], F32, name="cexp")
+        cexp = const.tile([P, 2 * M], F32, name="cexp")
         nc.vector.memset(cexp[:], -0.5)
-        cneg = const.tile([P, 2], F32, name="cneg")
+        cneg = const.tile([P, 2 * M], F32, name="cneg")
         nc.vector.memset(cneg[:], -1.0)
         cal = const.tile([P, 1], F32, name="cal")
         nc.vector.tensor_scalar(out=cal[:], in0=one[:], scalar1=-1.0 / ALPHA, scalar2=None, op0=ALU.mult)
-        ones = const.tile([P, 2], F32, name="ones")
+        ones = const.tile([P, 2 * M], F32, name="ones")
         nc.vector.memset(ones[:], 1.0)
         stt = []
         for i in range(NST):
-            st = const.tile([P, 2, 9], F32, name="st%d" % i)
+            st = const.tile([P, 2 * M, 9], F32, name="st%d" % i)
             nc.vector.memset(st[:], 0.0)
             nc.vector.tensor_scalar(out=st[:, :, 8], in0=ones[:], scalar1=H * EPS, scalar2=None, op0=ALU.mult)
             stt.append(st)
@@ -165,35 +166,42 @@ def tile_dynamicfeaturegroupinglayer_kernel(tc, x, W_masks, W1, W2, ln1_w, ln1_b
                 xs[g] = prepp.tile([P, M, B], U8, name="xs", tag="xs", align_bytes=64)
             nc.vector.quantize_mx(out=xc[g][:, m, :].bitcast(FP8X4), scales=xs[g][:, m, :], in_=wt[(g, m)][:])
 
-        mvt, rst, nrt, nbt = {}, {}, {}, {}
+        mvt, nrt, nbt, sbank = {}, {}, {}, {}
         hbank, zt, zbank, sig, r2, prod, finb = {}, {}, {}, {}, {}, {}, {}
 
-        def mx(t):
+        def mx(t, for_z):
             g, bh, m = t // 8, (t % 8) // 4, t % 4
             cols = slice(bh * P, (bh + 1) * P)
             for w in range(2):
-                bank = ph.tile([P, H], F32, name="h", tag="h")
+                if for_z:
+                    bank = ph.tile([P, H], F32, name="hz", tag="hz")
+                    hbank[(t, w)] = bank
+                else:
+                    bank = ps.tile([P, H], F32, name="hs", tag="hs")
+                    sbank[(t, w)] = bank
                 nc.tensor.matmul_mx(out=bank[:], lhsT=xc[g][:, m, cols].bitcast(FP8X4), lhsT_scale=xs[g][:, m, cols],
                                     rhs=wc[g][:, w, :].bitcast(FP8X4), rhs_scale=ws[g][:, w, :],
                                     start=True, stop=True)
-                hbank[(t, w)] = bank
 
         def bn(t):
             for w in range(2):
-                nc.vector.bn_stats(out=stt[t % NST][:, w, 0:6], in_=hbank[(t, w)][:])
+                nc.vector.bn_stats(out=stt[(t // M) % NST][:, 2 * (t % M) + w, 0:6], in_=sbank[(t, w)][:])
 
         def ag(t):
-            mvt[t] = small.tile([P, 2, 2], F32, name="mv", tag="mv")
+            ss = t // M
+            if ss not in mvt:
+                mvt[ss] = small.tile([P, 2 * M, 2], F32, name="mv", tag="mv")
             for w in range(2):
-                nc.vector.bn_aggr(out=mvt[t][:, w, :], in_=stt[t % NST][:, w, :])
+                i = 2 * (t % M) + w
+                nc.vector.bn_aggr(out=mvt[ss][:, i, :], in_=stt[ss % NST][:, i, :])
 
-        def chain(t):
-            rst[t] = small.tile([P, 2], F32, name="rs", tag="rs")
-            nc.gpsimd.tensor_tensor(out=rst[t][:], in0=mvt[t][:, :, 1], in1=cexp[:], op=ALU.pow)
-            nrt[t] = small.tile([P, 2], F32, name="nr", tag="nr")
-            nc.gpsimd.tensor_tensor(out=nrt[t][:], in0=rst[t][:], in1=cneg[:], op=ALU.mult)
-            nbt[t] = small.tile([P, 2], F32, name="nb", tag="nb")
-            nc.gpsimd.tensor_tensor(out=nbt[t][:], in0=mvt[t][:, :, 0], in1=rst[t][:], op=ALU.mult)
+        def chain(ss):
+            rs = small.tile([P, 2 * M], F32, name="rs", tag="rs")
+            nc.gpsimd.tensor_tensor(out=rs[:], in0=mvt[ss][:, :, 1], in1=cexp[:], op=ALU.pow)
+            nrt[ss] = small.tile([P, 2 * M], F32, name="nr", tag="nr")
+            nc.gpsimd.tensor_tensor(out=nrt[ss][:], in0=rs[:], in1=cneg[:], op=ALU.mult)
+            nbt[ss] = small.tile([P, 2 * M], F32, name="nb", tag="nb")
+            nc.gpsimd.tensor_tensor(out=nbt[ss][:], in0=mvt[ss][:, :, 0], in1=rs[:], op=ALU.mult)
 
         def z_dst(t, w):
             ss, m = t // 4, t % 4
@@ -202,12 +210,14 @@ def tile_dynamicfeaturegroupinglayer_kernel(tc, x, W_masks, W1, W2, ln1_w, ln1_b
             return zt[ss][:, w, m, :]
 
         def z_scalar(t, w):
+            ss, i = t // M, 2 * (t % M) + w
             nc.scalar.activation(out=z_dst(t, w), in_=hbank[(t, w)][:], func=ACT.Identity,
-                                 bias=nbt[t][:, w:w + 1], scale=nrt[t][:, w:w + 1])
+                                 bias=nbt[ss][:, i:i + 1], scale=nrt[ss][:, i:i + 1])
 
         def z_vector(t, w):
-            nc.vector.tensor_scalar(out=z_dst(t, w), in0=hbank[(t, w)][:], scalar1=mvt[t][:, w, 0:1],
-                                    scalar2=nrt[t][:, w:w + 1], op0=ALU.subtract, op1=ALU.mult)
+            ss, i = t // M, 2 * (t % M) + w
+            nc.vector.tensor_scalar(out=z_dst(t, w), in0=hbank[(t, w)][:], scalar1=mvt[ss][:, i, 0:1],
+                                    scalar2=nrt[ss][:, i:i + 1], op0=ALU.subtract, op1=ALU.mult)
 
         def tr(ss, k):
             jt, w = k // 2, k % 2
@@ -258,7 +268,10 @@ def tile_dynamicfeaturegroupinglayer_kernel(tc, x, W_masks, W1, W2, ln1_w, ln1_b
         mps = pz.tile([P, 4, P], F32, name="mps", tag="zT")
         x_t(0, pz, "zT")
         for f in range(4):
-            wfill_t(0, f, ph, "h")
+            if f < 2:
+                wfill_t(0, f, ps, "hs")
+            else:
+                wfill_t(0, f, ph, "hz")
             wfill_copy(0, f, True)
         for q in range(4):
             nc.tensor.transpose(mps[:, q, :], mask_sb[:, q:S:4], ident[:])
@@ -271,7 +284,7 @@ def tile_dynamicfeaturegroupinglayer_kernel(tc, x, W_masks, W1, W2, ln1_w, ln1_b
         weighted(0, 0)
         quant_w(0, 1)
         quant_x(0, 0)
-        mx(0)
+        mx(0, False)
         x_t(1, pz, "zT")
         wfill_t(1, 0, pprep, "prep")
         lnT = const.tile([P, 2, P], F32, name="lnT")
@@ -327,17 +340,21 @@ def tile_dynamicfeaturegroupinglayer_kernel(tc, x, W_masks, W1, W2, ln1_w, ln1_b
             elif k >= 4:
                 wfill_t(g, k - 4, pprep, "prep")
 
-        for t in range(NSTEP + 7):
-            tz = t - 1
+        for t in range(NSTEP + 11):
+            tz = t - 5
             ta = tz - 4
             tm = ta - 1
             tf = tm - 1
             if t % 8 == 0 and t // 8 + 2 < G:
                 load_w(t // 8 + 2)
+            if 0 <= tz < NSTEP:
+                mx(tz, True)
             if t < NSTEP:
                 bn(t)
                 ag(t)
                 prep_v(t)
+            if t + 1 < NSTEP:
+                mx(t + 1, False)
             if 0 <= ta < NSTEP:
                 tr(ta // 4, 2 * (ta % 4))
                 tr(ta // 4, 2 * (ta % 4) + 1)
@@ -349,8 +366,8 @@ def tile_dynamicfeaturegroupinglayer_kernel(tc, x, W_masks, W1, W2, ln1_w, ln1_b
                     z_vector(tz, 1)
             if 0 <= tm < NSTEP:
                 mul(tm // 4, tm % 4, t - 1 >= V_TAKES_RELU)
-            if t < NSTEP:
-                chain(t)
+            if t < NSTEP and t % M == M - 1:
+                chain(t // M)
             if 0 <= ta < NSTEP:
                 act_sig(ta // 4, ta % 4)
                 act_relu(ta // 4, ta % 4, t >= V_TAKES_RELU)
@@ -359,7 +376,5 @@ def tile_dynamicfeaturegroupinglayer_kernel(tc, x, W_masks, W1, W2, ln1_w, ln1_b
                 if tf % 4 == 3:
                     fin(tf // 4)
             prep_s(t)
-            if t + 1 < NSTEP:
-                mx(t + 1)
             if t < NSTEP:
                 prep_pe(t)

@@ -23,6 +23,7 @@ NSS = G * 2
 GM = G * M
 V_TAKES_Z = 8 * (G - 1)
 V_TAKES_RELU = NSTEP
+T_PAIR = NSTEP + 5
 NST = 2
 
 
@@ -33,10 +34,11 @@ def tile_dynamicfeaturegroupinglayer_kernel(tc, x, W_masks, W1, W2, ln1_w, ln1_b
         const = ctx.enter_context(tc.tile_pool(name="const", bufs=1))
         wrawp = ctx.enter_context(tc.tile_pool(name="wrawp", bufs=3))
         prepp = ctx.enter_context(tc.tile_pool(name="prepp", bufs=2))
+        qp = ctx.enter_context(tc.tile_pool(name="qp", bufs=3))
         wtp = ctx.enter_context(tc.tile_pool(name="wtp", bufs=4))
         small = ctx.enter_context(tc.tile_pool(name="small", bufs=4))
         zp = ctx.enter_context(tc.tile_pool(name="zp", bufs=2))
-        ap3 = ctx.enter_context(tc.tile_pool(name="ap3", bufs=3))
+        ap3 = ctx.enter_context(tc.tile_pool(name="ap3", bufs=4))
         outp = ctx.enter_context(tc.tile_pool(name="outp", bufs=2))
         ps = ctx.enter_context(tc.psum_pool(name="ps", bufs=2))
         ph = ctx.enter_context(tc.psum_pool(name="ph", bufs=2))
@@ -110,10 +112,6 @@ def tile_dynamicfeaturegroupinglayer_kernel(tc, x, W_masks, W1, W2, ln1_w, ln1_b
         nc.vector.tensor_scalar(out=sae[0:GM, :], in0=sa[0:GM, :], scalar1=EPS, scalar2=None, op0=ALU.add)
         msc = const.tile([P, 1], F32, name="msc")
         nc.gpsimd.tensor_tensor(out=msc[0:GM, :], in0=sae[0:GM, :], in1=cal[0:GM, :], op=ALU.pow)
-        nc.vector.tensor_scalar(out=mask_sb[0:GM, :], in0=e_sb[0:GM, :], scalar1=msc[0:GM, :], scalar2=None,
-                                op0=ALU.mult)
-        lnf = const.tile([P, 2, P], F32, name="lnf")
-        nc.vector.tensor_copy(out=lnf[:], in_=lnraw[:])
 
         gw, wc, ws, xc, xs, xbank, wt, fillb = {}, {}, {}, {}, {}, {}, {}, {}
 
@@ -139,8 +137,8 @@ def tile_dynamicfeaturegroupinglayer_kernel(tc, x, W_masks, W1, W2, ln1_w, ln1_b
 
         def quant_w(g, w):
             if w == 0:
-                wc[g] = prepp.tile([P, 2, H], U32, name="wc", tag="wc", align_bytes=64)
-                ws[g] = prepp.tile([P, 2, H], U8, name="ws", tag="ws", align_bytes=64)
+                wc[g] = qp.tile([P, 2, H], U32, name="wc", tag="wc", align_bytes=64)
+                ws[g] = qp.tile([P, 2, H], U8, name="ws", tag="ws", align_bytes=64)
             nc.vector.quantize_mx(out=wc[g][:, w, :].bitcast(FP8X4), scales=ws[g][:, w, :], in_=gw[(g, w)][:])
 
         def x_t(g, pool, tag):
@@ -162,12 +160,12 @@ def tile_dynamicfeaturegroupinglayer_kernel(tc, x, W_masks, W1, W2, ln1_w, ln1_b
 
         def quant_x(g, m):
             if m == 0:
-                xc[g] = prepp.tile([P, M, B], U32, name="xc", tag="xc", align_bytes=64)
-                xs[g] = prepp.tile([P, M, B], U8, name="xs", tag="xs", align_bytes=64)
+                xc[g] = qp.tile([P, M, B], U32, name="xc", tag="xc", align_bytes=64)
+                xs[g] = qp.tile([P, M, B], U8, name="xs", tag="xs", align_bytes=64)
             nc.vector.quantize_mx(out=xc[g][:, m, :].bitcast(FP8X4), scales=xs[g][:, m, :], in_=wt[(g, m)][:])
 
-        mvt, nrt, nbt, sbank = {}, {}, {}, {}
-        hbank, zt, zbank, sig, r2, prod, finb = {}, {}, {}, {}, {}, {}, {}
+        mvt, nrt, nbt = {}, {}, {}
+        hbank, zt, zbank, sig, r2, prod, half, finb = {}, {}, {}, {}, {}, {}, {}, {}
 
         def mx(t, for_z):
             g, bh, m = t // 8, (t % 8) // 4, t % 4
@@ -175,17 +173,16 @@ def tile_dynamicfeaturegroupinglayer_kernel(tc, x, W_masks, W1, W2, ln1_w, ln1_b
             for w in range(2):
                 if for_z:
                     bank = ph.tile([P, H], F32, name="hz", tag="hz")
-                    hbank[(t, w)] = bank
                 else:
                     bank = ps.tile([P, H], F32, name="hs", tag="hs")
-                    sbank[(t, w)] = bank
+                hbank[(t, w)] = bank
                 nc.tensor.matmul_mx(out=bank[:], lhsT=xc[g][:, m, cols].bitcast(FP8X4), lhsT_scale=xs[g][:, m, cols],
                                     rhs=wc[g][:, w, :].bitcast(FP8X4), rhs_scale=ws[g][:, w, :],
                                     start=True, stop=True)
 
         def bn(t):
             for w in range(2):
-                nc.vector.bn_stats(out=stt[(t // M) % NST][:, 2 * (t % M) + w, 0:6], in_=sbank[(t, w)][:])
+                nc.vector.bn_stats(out=stt[(t // M) % NST][:, 2 * (t % M) + w, 0:6], in_=hbank[(t, w)][:])
 
         def ag(t):
             ss = t // M
@@ -219,9 +216,12 @@ def tile_dynamicfeaturegroupinglayer_kernel(tc, x, W_masks, W1, W2, ln1_w, ln1_b
             nc.vector.tensor_scalar(out=z_dst(t, w), in0=hbank[(t, w)][:], scalar1=mvt[ss][:, i, 0:1],
                                     scalar2=nrt[ss][:, i:i + 1], op0=ALU.subtract, op1=ALU.mult)
 
-        def tr(ss, k):
+        def tr(ss, k, own):
             jt, w = k // 2, k % 2
-            bank = pz.tile([P, M, P], F32, name="zT", tag="zT")
+            if own:
+                bank = pz.tile([P, M, P], F32, name="zT", tag="zT")
+            else:
+                bank = ph.tile([P, M, P], F32, name="zTh", tag="hz")
             for m in range(M):
                 nc.tensor.transpose(bank[:, m, :], zt[ss][:, w, m, jt * P:(jt + 1) * P], ident[:])
             zbank[(ss, k)] = bank
@@ -252,12 +252,19 @@ def tile_dynamicfeaturegroupinglayer_kernel(tc, x, W_masks, W1, W2, ln1_w, ln1_b
             else:
                 nc.gpsimd.tensor_tensor(out=dst, in0=sig[(ss, jt)][:], in1=r2[(ss, jt)][:], op=ALU.mult)
 
+        def pair(ss, jt):
+            half[(ss, jt)] = ap3.tile([P, M // 2, P], F32, name="half", tag="half")
+            nc.gpsimd.tensor_tensor(out=half[(ss, jt)][:], in0=prod[(ss, jt)][:, 0:M // 2, :],
+                                    in1=prod[(ss, jt)][:, M // 2:M, :], op=ALU.add)
+
         def acc(ss, jt):
             if jt == 0:
                 finb[ss] = pfin.tile([P, H], F32, name="fin", tag="fin")
-            for m in range(M):
-                nc.tensor.matmul(finb[ss][:, jt * P:(jt + 1) * P], lhsT=prod[(ss, jt)][:, m, :], rhs=ident[:],
-                                 is_transpose=True, start=(m == 0), stop=(m == M - 1))
+            parts = half.get((ss, jt), prod[(ss, jt)])
+            n = parts.shape[1]
+            for m in range(n):
+                nc.tensor.matmul(finb[ss][:, jt * P:(jt + 1) * P], lhsT=parts[:, m, :], rhs=ident[:],
+                                 is_transpose=True, start=(m == 0), stop=(m == n - 1))
 
         def fin(ss):
             g, bh = ss // 2, ss % 2
@@ -272,41 +279,56 @@ def tile_dynamicfeaturegroupinglayer_kernel(tc, x, W_masks, W1, W2, ln1_w, ln1_b
                 wfill_t(0, f, ps, "hs")
             else:
                 wfill_t(0, f, ph, "hz")
-            wfill_copy(0, f, True)
+            wfill_copy(0, f, f >= 2)
+        nc.vector.tensor_scalar(out=mask_sb[0:GM, :], in0=e_sb[0:GM, :], scalar1=msc[0:GM, :], scalar2=None,
+                                op0=ALU.mult)
+        quant_w(0, 0)
         for q in range(4):
             nc.tensor.transpose(mps[:, q, :], mask_sb[:, q:S:4], ident[:])
-        lps = pfin.tile([P, 2, P], F32, name="lps", tag="fin")
-        for a in range(2):
-            nc.tensor.transpose(lps[:, a, :], lnf[:, a, :], ident[:])
-        quant_w(0, 0)
         maskT = const.tile([P, GM, 4], F32, name="maskT")
         nc.vector.tensor_copy(out=maskT[:], in_=mps[:, :, 0:GM].rearrange("p t c -> p c t"))
-        weighted(0, 0)
         quant_w(0, 1)
+        weighted(0, 0)
+        x_t(1, pz, "zT")
+        weighted(0, 1)
         quant_x(0, 0)
         mx(0, False)
-        x_t(1, pz, "zT")
         wfill_t(1, 0, pprep, "prep")
+        lnf = const.tile([P, 2, P], F32, name="lnf")
         lnT = const.tile([P, 2, P], F32, name="lnT")
-        weighted(0, 1)
-        nc.vector.tensor_scalar(out=lnT[:, :, 0:GM], in0=lps[:, :, 0:GM], scalar1=-1.0, scalar2=None, op0=ALU.mult)
-        nc.vector.tensor_copy(out=lnT[:, :, GM:2 * GM], in_=lps[:, :, GM:2 * GM])
-        quant_x(0, 1)
+
+        def ln_in():
+            nc.vector.tensor_copy(out=lnf[:], in_=lnraw[:])
+
+        def ln_t():
+            lps = pfin.tile([P, 2, P], F32, name="lps", tag="fin")
+            for a in range(2):
+                nc.tensor.transpose(lps[:, a, :], lnf[:, a, :], ident[:])
+            nc.vector.tensor_scalar(out=lnT[:, :, 0:GM], in0=lps[:, :, 0:GM], scalar1=-1.0, scalar2=None, op0=ALU.mult)
+            nc.vector.tensor_copy(out=lnT[:, :, GM:2 * GM], in_=lps[:, :, GM:2 * GM])
 
         def prep_v(t):
-            if t < 2:
-                weighted(0, t + 2)
-                if t == 1:
-                    weighted(1, 0)
-                quant_x(0, t + 2)
+            if t == 0:
+                quant_x(0, 1)
+                weighted(0, 2)
+            elif t == 1:
+                quant_x(0, 2)
+                weighted(0, 3)
+                weighted(1, 0)
+            elif t == 2:
+                quant_x(0, 3)
+                quant_x(1, 0)
+                weighted(1, 1)
+                ln_in()
             elif t < 5:
-                weighted(1, t - 1)
                 quant_x(1, t - 2)
+                weighted(1, t - 1)
             elif t == 5:
-                quant_x(1, 3)
                 quant_w(1, 0)
+                quant_x(1, 3)
             elif t == 6:
                 quant_w(1, 1)
+                ln_t()
             g, k = (t + 1) // 8 + 1, (t + 1) % 8
             if g < 2 or g >= G:
                 return
@@ -339,42 +361,51 @@ def tile_dynamicfeaturegroupinglayer_kernel(tc, x, W_masks, W1, W2, ln1_w, ln1_b
                 x_t(g, pprep, "prep")
             elif k >= 4:
                 wfill_t(g, k - 4, pprep, "prep")
-
         for t in range(NSTEP + 11):
-            tz = t - 5
-            ta = tz - 4
+            ta = t - 9
             tm = ta - 1
-            tf = tm - 1
+            tp = tm - 1
+            if t < NSTEP:
+                zs = [(t - 5, True)] if t >= 5 else []
+            else:
+                zs = [(i, i % 2 == NSTEP % 2 + 1) for i in range(NSTEP - 5 + 2 * (t - NSTEP), min(NSTEP, NSTEP - 3 + 2 * (t - NSTEP)))]
+            zvec = 0 if t < V_TAKES_Z else 1
             if t % 8 == 0 and t // 8 + 2 < G:
                 load_w(t // 8 + 2)
-            if 0 <= tz < NSTEP:
-                mx(tz, True)
+            for i, b in zs:
+                mx(i, b)
             if t < NSTEP:
                 bn(t)
-                ag(t)
+            if t < NSTEP:
                 prep_v(t)
+            for i, b in zs:
+                for w in range(2):
+                    if w < 2 - zvec:
+                        z_scalar(i, w)
+                    else:
+                        z_vector(i, w)
+            if t < NSTEP:
+                ag(t)
             if t + 1 < NSTEP:
                 mx(t + 1, False)
             if 0 <= ta < NSTEP:
-                tr(ta // 4, 2 * (ta % 4))
-                tr(ta // 4, 2 * (ta % 4) + 1)
-            if 0 <= tz < NSTEP:
-                z_scalar(tz, 0)
-                if t < V_TAKES_Z:
-                    z_scalar(tz, 1)
-                else:
-                    z_vector(tz, 1)
+                own = t < NSTEP + 3 or t % 2 == 0
+                tr(ta // 4, 2 * (ta % 4), own)
+                tr(ta // 4, 2 * (ta % 4) + 1, own)
+            if 0 <= tp < NSTEP and t < T_PAIR and (t % M != M - 1 or t >= NSTEP):
+                pair(tp // 4, tp % 4)
             if 0 <= tm < NSTEP:
-                mul(tm // 4, tm % 4, t - 1 >= V_TAKES_RELU)
+                mul(tm // 4, tm % 4, t >= V_TAKES_RELU)
             if t < NSTEP and t % M == M - 1:
                 chain(t // M)
             if 0 <= ta < NSTEP:
                 act_sig(ta // 4, ta % 4)
-                act_relu(ta // 4, ta % 4, t >= V_TAKES_RELU)
-            if 0 <= tf < NSTEP:
-                acc(tf // 4, tf % 4)
-                if tf % 4 == 3:
-                    fin(tf // 4)
+                act_relu(ta // 4, ta % 4, t >= V_TAKES_RELU and t % 2 == 0)
+            for tf in ((t - 12,) if t < T_PAIR else (t - 12, t - 11) if t == T_PAIR else (t - 11,)):
+                if 0 <= tf < NSTEP:
+                    acc(tf // 4, tf % 4)
+                    if tf % 4 == 3:
+                        fin(tf // 4)
             prep_s(t)
             if t < NSTEP:
                 prep_pe(t)

@@ -23,7 +23,6 @@ NSS = G * 2
 GM = G * M
 V_TAKES_Z = 8 * (G - 1)
 V_TAKES_RELU = NSTEP
-T_PAIR = NSTEP + 5
 NST = 2
 
 
@@ -165,7 +164,7 @@ def tile_dynamicfeaturegroupinglayer_kernel(tc, x, W_masks, W1, W2, ln1_w, ln1_b
             nc.vector.quantize_mx(out=xc[g][:, m, :].bitcast(FP8X4), scales=xs[g][:, m, :], in_=wt[(g, m)][:])
 
         mvt, nrt, nbt = {}, {}, {}
-        hbank, zt, zbank, sig, r2, prod, half, finb = {}, {}, {}, {}, {}, {}, {}, {}
+        hbank, zt, zbank, sig, r2, prod, finb = {}, {}, {}, {}, {}, {}, {}
 
         def mx(t, for_z):
             g, bh, m = t // 8, (t % 8) // 4, t % 4
@@ -252,19 +251,12 @@ def tile_dynamicfeaturegroupinglayer_kernel(tc, x, W_masks, W1, W2, ln1_w, ln1_b
             else:
                 nc.gpsimd.tensor_tensor(out=dst, in0=sig[(ss, jt)][:], in1=r2[(ss, jt)][:], op=ALU.mult)
 
-        def pair(ss, jt):
-            half[(ss, jt)] = ap3.tile([P, M // 2, P], F32, name="half", tag="half")
-            nc.gpsimd.tensor_tensor(out=half[(ss, jt)][:], in0=prod[(ss, jt)][:, 0:M // 2, :],
-                                    in1=prod[(ss, jt)][:, M // 2:M, :], op=ALU.add)
-
         def acc(ss, jt):
             if jt == 0:
                 finb[ss] = pfin.tile([P, H], F32, name="fin", tag="fin")
-            parts = half.get((ss, jt), prod[(ss, jt)])
-            n = parts.shape[1]
-            for m in range(n):
-                nc.tensor.matmul(finb[ss][:, jt * P:(jt + 1) * P], lhsT=parts[:, m, :], rhs=ident[:],
-                                 is_transpose=True, start=(m == 0), stop=(m == n - 1))
+            for m in range(M):
+                nc.tensor.matmul(finb[ss][:, jt * P:(jt + 1) * P], lhsT=prod[(ss, jt)][:, m, :], rhs=ident[:],
+                                 is_transpose=True, start=(m == 0), stop=(m == M - 1))
 
         def fin(ss):
             g, bh = ss // 2, ss % 2
@@ -364,7 +356,7 @@ def tile_dynamicfeaturegroupinglayer_kernel(tc, x, W_masks, W1, W2, ln1_w, ln1_b
         for t in range(NSTEP + 11):
             ta = t - 9
             tm = ta - 1
-            tp = tm - 1
+            tf = tm - 1
             if t < NSTEP:
                 zs = [(t - 5, True)] if t >= 5 else []
             else:
@@ -388,12 +380,12 @@ def tile_dynamicfeaturegroupinglayer_kernel(tc, x, W_masks, W1, W2, ln1_w, ln1_b
                 ag(t)
             if t + 1 < NSTEP:
                 mx(t + 1, False)
+            if t < NSTEP:
+                prep_pe(t)
             if 0 <= ta < NSTEP:
                 own = t < NSTEP + 3 or t % 2 == 0
                 tr(ta // 4, 2 * (ta % 4), own)
                 tr(ta // 4, 2 * (ta % 4) + 1, own)
-            if 0 <= tp < NSTEP and t < T_PAIR and (t % M != M - 1 or t >= NSTEP):
-                pair(tp // 4, tp % 4)
             if 0 <= tm < NSTEP:
                 mul(tm // 4, tm % 4, t >= V_TAKES_RELU)
             if t < NSTEP and t % M == M - 1:
@@ -401,11 +393,8 @@ def tile_dynamicfeaturegroupinglayer_kernel(tc, x, W_masks, W1, W2, ln1_w, ln1_b
             if 0 <= ta < NSTEP:
                 act_sig(ta // 4, ta % 4)
                 act_relu(ta // 4, ta % 4, t >= V_TAKES_RELU and t % 2 == 0)
-            for tf in ((t - 12,) if t < T_PAIR else (t - 12, t - 11) if t == T_PAIR else (t - 11,)):
-                if 0 <= tf < NSTEP:
-                    acc(tf // 4, tf % 4)
-                    if tf % 4 == 3:
-                        fin(tf // 4)
+            if 0 <= tf < NSTEP:
+                acc(tf // 4, tf % 4)
+                if tf % 4 == 3:
+                    fin(tf // 4)
             prep_s(t)
-            if t < NSTEP:
-                prep_pe(t)

@@ -23,6 +23,8 @@ NSS = G * 2
 GM = G * M
 V_TAKES_Z = 8 * (G - 1)
 V_TAKES_RELU = NSTEP
+PAIR = True
+RV = False
 NST = 2
 
 
@@ -34,8 +36,8 @@ def tile_dynamicfeaturegroupinglayer_kernel(tc, x, W_masks, W1, W2, ln1_w, ln1_b
         wrawp = ctx.enter_context(tc.tile_pool(name="wrawp", bufs=3))
         prepp = ctx.enter_context(tc.tile_pool(name="prepp", bufs=2))
         qp = ctx.enter_context(tc.tile_pool(name="qp", bufs=3))
-        wtp = ctx.enter_context(tc.tile_pool(name="wtp", bufs=4))
-        small = ctx.enter_context(tc.tile_pool(name="small", bufs=4))
+        wtp = ctx.enter_context(tc.tile_pool(name="wtp", bufs=8))
+        small = ctx.enter_context(tc.tile_pool(name="small", bufs=5))
         zp = ctx.enter_context(tc.tile_pool(name="zp", bufs=2))
         ap3 = ctx.enter_context(tc.tile_pool(name="ap3", bufs=4))
         outp = ctx.enter_context(tc.tile_pool(name="outp", bufs=2))
@@ -78,17 +80,17 @@ def tile_dynamicfeaturegroupinglayer_kernel(tc, x, W_masks, W1, W2, ln1_w, ln1_b
         nc.vector.memset(one[:], 1.0)
         warm = const.tile([P, 1], F32, name="warm")
         nc.scalar.activation(out=warm[:], in_=one[:], func=ACT.Exp)
-        cexp = const.tile([P, 2 * M], F32, name="cexp")
+        cexp = const.tile([P, 4], F32, name="cexp")
         nc.vector.memset(cexp[:], -0.5)
-        cneg = const.tile([P, 2 * M], F32, name="cneg")
+        cneg = const.tile([P, 4], F32, name="cneg")
         nc.vector.memset(cneg[:], -1.0)
         cal = const.tile([P, 1], F32, name="cal")
         nc.vector.tensor_scalar(out=cal[:], in0=one[:], scalar1=-1.0 / ALPHA, scalar2=None, op0=ALU.mult)
-        ones = const.tile([P, 2 * M], F32, name="ones")
+        ones = const.tile([P, 4], F32, name="ones")
         nc.vector.memset(ones[:], 1.0)
         stt = []
         for i in range(NST):
-            st = const.tile([P, 2 * M, 9], F32, name="st%d" % i)
+            st = const.tile([P, 4, 9], F32, name="st%d" % i)
             nc.vector.memset(st[:], 0.0)
             nc.vector.tensor_scalar(out=st[:, :, 8], in0=ones[:], scalar1=H * EPS, scalar2=None, op0=ALU.mult)
             stt.append(st)
@@ -97,16 +99,17 @@ def tile_dynamicfeaturegroupinglayer_kernel(tc, x, W_masks, W1, W2, ln1_w, ln1_b
 
         mx_ = const.tile([P, 1], F32, name="mx_")
         nc.vector.reduce_max(out=mx_[0:GM, :], in_=wm[0:GM, :], axis=AX.X)
-        nmx = const.tile([P, 1], F32, name="nmx")
-        nc.vector.tensor_scalar(out=nmx[0:GM, :], in0=mx_[0:GM, :], scalar1=-1.0, scalar2=None, op0=ALU.mult)
         nmxa = const.tile([P, 1], F32, name="nmxa")
-        nc.vector.tensor_scalar(out=nmxa[0:GM, :], in0=mx_[0:GM, :], scalar1=-ALPHA, scalar2=None, op0=ALU.mult)
+        nc.scalar.mul(out=nmxa[0:GM, :], in_=mx_[0:GM, :], mul=-ALPHA)
+        nmx = const.tile([P, 1], F32, name="nmx")
+        nc.scalar.mul(out=nmx[0:GM, :], in_=mx_[0:GM, :], mul=-1.0)
         ea_sb = const.tile([P, S], F32, name="ea_sb")
         sa = const.tile([P, 1], F32, name="sa")
         nc.scalar.activation(out=ea_sb[0:GM, :], in_=wm[0:GM, :], func=ACT.Exp, bias=nmxa[0:GM, :], scale=ALPHA,
                              accum_out=sa[0:GM, :])
         e_sb = const.tile([P, S], F32, name="e_sb")
         nc.scalar.activation(out=e_sb[0:GM, :], in_=wm[0:GM, :], func=ACT.Exp, bias=nmx[0:GM, :], scale=1.0)
+        nc.scalar.activation(out=warm[:], in_=one[:], func=ACT.Sigmoid)
         sae = const.tile([P, 1], F32, name="sae")
         nc.vector.tensor_scalar(out=sae[0:GM, :], in0=sa[0:GM, :], scalar1=EPS, scalar2=None, op0=ALU.add)
         msc = const.tile([P, 1], F32, name="msc")
@@ -149,19 +152,20 @@ def tile_dynamicfeaturegroupinglayer_kernel(tc, x, W_masks, W1, W2, ln1_w, ln1_b
                                         src[:, 256 * g + u:256 * (g + 1):2], ident[:])
             xbank[g] = bank
 
-        def weighted(g, m):
-            t_ = wtp.tile([P, 4 * B], BF16, name="wt", tag="wt", align_bytes=64)
+        def weighted(g, m, lo=0, hi=B):
+            if lo == 0:
+                wt[(g, m)] = wtp.tile([P, 4 * B], BF16, name="wt", tag="wt", align_bytes=64)
             in0 = xbank[g][:].rearrange("p u b -> p (u b)").bitcast(BF16).rearrange("p (u b e) -> p b u e", u=2, e=2)
-            in1 = maskT[:, g * M + m, :].rearrange("p (u e) -> p u e", u=2).unsqueeze(1).to_broadcast([P, B, 2, 2])
-            nc.vector.tensor_tensor(out=t_[:].rearrange("p (b u e) -> p b u e", u=2, e=2), in0=in0, in1=in1,
-                                    op=ALU.mult)
-            wt[(g, m)] = t_
+            in1 = maskT[:, g * M + m, :].rearrange("p (u e) -> p u e", u=2).unsqueeze(1)
+            nc.vector.tensor_tensor(out=wt[(g, m)][:, 4 * lo:4 * hi].rearrange("p (b u e) -> p b u e", u=2, e=2),
+                                    in0=in0[:, lo:hi], in1=in1.to_broadcast([P, hi - lo, 2, 2]), op=ALU.mult)
 
-        def quant_x(g, m):
-            if m == 0:
+        def quant_x(g, m, lo=0, hi=B):
+            if g not in xc:
                 xc[g] = qp.tile([P, M, B], U32, name="xc", tag="xc", align_bytes=64)
                 xs[g] = qp.tile([P, M, B], U8, name="xs", tag="xs", align_bytes=64)
-            nc.vector.quantize_mx(out=xc[g][:, m, :].bitcast(FP8X4), scales=xs[g][:, m, :], in_=wt[(g, m)][:])
+            nc.vector.quantize_mx(out=xc[g][:, m, lo:hi].bitcast(FP8X4), scales=xs[g][:, m, lo:hi],
+                                  in_=wt[(g, m)][:, 4 * lo:4 * hi])
 
         mvt, nrt, nbt = {}, {}, {}
         hbank, zt, zbank, sig, r2, prod, finb = {}, {}, {}, {}, {}, {}, {}
@@ -181,22 +185,22 @@ def tile_dynamicfeaturegroupinglayer_kernel(tc, x, W_masks, W1, W2, ln1_w, ln1_b
 
         def bn(t):
             for w in range(2):
-                nc.vector.bn_stats(out=stt[(t // M) % NST][:, 2 * (t % M) + w, 0:6], in_=hbank[(t, w)][:])
+                nc.vector.bn_stats(out=stt[(t // 2) % NST][:, 2 * (t % 2) + w, 0:6], in_=hbank[(t, w)][:])
 
         def ag(t):
-            ss = t // M
+            ss = t // 2
             if ss not in mvt:
-                mvt[ss] = small.tile([P, 2 * M, 2], F32, name="mv", tag="mv")
+                mvt[ss] = small.tile([P, 4, 2], F32, name="mv", tag="mv")
             for w in range(2):
-                i = 2 * (t % M) + w
+                i = 2 * (t % 2) + w
                 nc.vector.bn_aggr(out=mvt[ss][:, i, :], in_=stt[ss % NST][:, i, :])
 
         def chain(ss):
-            rs = small.tile([P, 2 * M], F32, name="rs", tag="rs")
+            rs = small.tile([P, 4], F32, name="rs", tag="rs")
             nc.gpsimd.tensor_tensor(out=rs[:], in0=mvt[ss][:, :, 1], in1=cexp[:], op=ALU.pow)
-            nrt[ss] = small.tile([P, 2 * M], F32, name="nr", tag="nr")
+            nrt[ss] = small.tile([P, 4], F32, name="nr", tag="nr")
             nc.gpsimd.tensor_tensor(out=nrt[ss][:], in0=rs[:], in1=cneg[:], op=ALU.mult)
-            nbt[ss] = small.tile([P, 2 * M], F32, name="nb", tag="nb")
+            nbt[ss] = small.tile([P, 4], F32, name="nb", tag="nb")
             nc.gpsimd.tensor_tensor(out=nbt[ss][:], in0=mvt[ss][:, :, 0], in1=rs[:], op=ALU.mult)
 
         def z_dst(t, w):
@@ -206,12 +210,12 @@ def tile_dynamicfeaturegroupinglayer_kernel(tc, x, W_masks, W1, W2, ln1_w, ln1_b
             return zt[ss][:, w, m, :]
 
         def z_scalar(t, w):
-            ss, i = t // M, 2 * (t % M) + w
+            ss, i = t // 2, 2 * (t % 2) + w
             nc.scalar.activation(out=z_dst(t, w), in_=hbank[(t, w)][:], func=ACT.Identity,
                                  bias=nbt[ss][:, i:i + 1], scale=nrt[ss][:, i:i + 1])
 
         def z_vector(t, w):
-            ss, i = t // M, 2 * (t % M) + w
+            ss, i = t // 2, 2 * (t % 2) + w
             nc.vector.tensor_scalar(out=z_dst(t, w), in0=hbank[(t, w)][:], scalar1=mvt[ss][:, i, 0:1],
                                     scalar2=nrt[ss][:, i:i + 1], op0=ALU.subtract, op1=ALU.mult)
 
@@ -275,15 +279,15 @@ def tile_dynamicfeaturegroupinglayer_kernel(tc, x, W_masks, W1, W2, ln1_w, ln1_b
         nc.vector.tensor_scalar(out=mask_sb[0:GM, :], in0=e_sb[0:GM, :], scalar1=msc[0:GM, :], scalar2=None,
                                 op0=ALU.mult)
         quant_w(0, 0)
+        quant_w(0, 1)
         for q in range(4):
             nc.tensor.transpose(mps[:, q, :], mask_sb[:, q:S:4], ident[:])
         maskT = const.tile([P, GM, 4], F32, name="maskT")
         nc.vector.tensor_copy(out=maskT[:], in_=mps[:, :, 0:GM].rearrange("p t c -> p c t"))
-        quant_w(0, 1)
-        weighted(0, 0)
+        weighted(0, 0, 0, P)
         x_t(1, pz, "zT")
-        weighted(0, 1)
-        quant_x(0, 0)
+        weighted(0, 1, 0, P)
+        quant_x(0, 0, 0, P)
         mx(0, False)
         wfill_t(1, 0, pprep, "prep")
         lnf = const.tile([P, 2, P], F32, name="lnf")
@@ -300,26 +304,26 @@ def tile_dynamicfeaturegroupinglayer_kernel(tc, x, W_masks, W1, W2, ln1_w, ln1_b
             nc.vector.tensor_copy(out=lnT[:, :, GM:2 * GM], in_=lps[:, :, GM:2 * GM])
 
         def prep_v(t):
-            if t == 0:
-                quant_x(0, 1)
-                weighted(0, 2)
-            elif t == 1:
-                quant_x(0, 2)
-                weighted(0, 3)
-                weighted(1, 0)
+            if t < 3:
+                quant_x(0, t + 1, 0, P)
+            elif t < 6:
+                quant_x(0, t - 2, P, B)
+            if t < 2:
+                weighted(0, t + 2, 0, P)
+                weighted(0, t, P, B)
             elif t == 2:
-                quant_x(0, 3)
-                quant_x(1, 0)
-                weighted(1, 1)
+                weighted(0, 2, P, B)
+                weighted(0, 3, P, B)
+                quant_x(0, 0, P, B)
+            elif t < 7:
+                weighted(1, t - 3)
+            if 5 <= t < 7:
+                quant_w(1, t - 5)
+            if 5 <= t < 9:
+                quant_x(1, t - 5)
+            if t == 4:
                 ln_in()
-            elif t < 5:
-                quant_x(1, t - 2)
-                weighted(1, t - 1)
             elif t == 5:
-                quant_w(1, 0)
-                quant_x(1, 3)
-            elif t == 6:
-                quant_w(1, 1)
                 ln_t()
             g, k = (t + 1) // 8 + 1, (t + 1) % 8
             if g < 2 or g >= G:
@@ -353,15 +357,13 @@ def tile_dynamicfeaturegroupinglayer_kernel(tc, x, W_masks, W1, W2, ln1_w, ln1_b
                 x_t(g, pprep, "prep")
             elif k >= 4:
                 wfill_t(g, k - 4, pprep, "prep")
-        for t in range(NSTEP + 11):
-            ta = t - 9
+        for t in range(NSTEP + 9):
+            ta = t - 7
             tm = ta - 1
-            tf = tm - 1
-            if t < NSTEP:
-                zs = [(t - 5, True)] if t >= 5 else []
-            else:
-                zs = [(i, i % 2 == NSTEP % 2 + 1) for i in range(NSTEP - 5 + 2 * (t - NSTEP), min(NSTEP, NSTEP - 3 + 2 * (t - NSTEP)))]
+            tf = t - 9
+            zs = [(t - 3, True)] if 0 <= t - 3 < NSTEP else []
             zvec = 0 if t < V_TAKES_Z else 1
+            own = t < NSTEP + 3 or t % 2 == 0
             if t % 8 == 0 and t // 8 + 2 < G:
                 load_w(t // 8 + 2)
             for i, b in zs:
@@ -388,13 +390,13 @@ def tile_dynamicfeaturegroupinglayer_kernel(tc, x, W_masks, W1, W2, ln1_w, ln1_b
                 tr(ta // 4, 2 * (ta % 4) + 1, own)
             if 0 <= tm < NSTEP:
                 mul(tm // 4, tm % 4, t >= V_TAKES_RELU)
-            if t < NSTEP and t % M == M - 1:
-                chain(t // M)
+            if t < NSTEP and t % 2 == 1:
+                chain(t // 2)
             if 0 <= ta < NSTEP:
                 act_sig(ta // 4, ta % 4)
-                act_relu(ta // 4, ta % 4, t >= V_TAKES_RELU and t % 2 == 0)
+                act_relu(ta // 4, ta % 4, t > V_TAKES_RELU and t % 2 == 1)
             if 0 <= tf < NSTEP:
                 acc(tf // 4, tf % 4)
-                if tf % 4 == 3:
-                    fin(tf // 4)
+            if 0 <= tf < NSTEP and tf % 4 == 3:
+                fin(tf // 4)
             prep_s(t)

@@ -19,12 +19,9 @@ P = 128
 FLOPS = 2 * 2 * B * G * M * S * H
 
 NSTEP = G * 2 * M
-NSS = G * 2
 GM = G * M
 V_TAKES_Z = 8 * (G - 1)
 V_TAKES_RELU = NSTEP
-PAIR = True
-RV = False
 NST = 2
 
 
@@ -94,7 +91,7 @@ def tile_dynamicfeaturegroupinglayer_kernel(tc, x, W_masks, W1, W2, ln1_w, ln1_b
             nc.vector.memset(st[:], 0.0)
             nc.vector.tensor_scalar(out=st[:, :, 8], in0=ones[:], scalar1=H * EPS, scalar2=None, op0=ALU.mult)
             stt.append(st)
-        mask_sb = const.tile([P, S], F32, name="mask_sb")
+        mask_sb = const.tile([P, 4, P], F32, name="mask_sb")
         nc.vector.memset(mask_sb[:], 0.0)
 
         mx_ = const.tile([P, 1], F32, name="mx_")
@@ -159,6 +156,14 @@ def tile_dynamicfeaturegroupinglayer_kernel(tc, x, W_masks, W1, W2, ln1_w, ln1_b
             in1 = maskT[:, g * M + m, :].rearrange("p (u e) -> p u e", u=2).unsqueeze(1)
             nc.vector.tensor_tensor(out=wt[(g, m)][:, 4 * lo:4 * hi].rearrange("p (b u e) -> p b u e", u=2, e=2),
                                     in0=in0[:, lo:hi], in1=in1.to_broadcast([P, hi - lo, 2, 2]), op=ALU.mult)
+
+        def weighted_s(g, m, q):
+            if q == 0:
+                wt[(g, m)] = wtp.tile([P, 4 * B], BF16, name="wt", tag="wt", align_bytes=64)
+            src = xbank[g][:].rearrange("p u b -> p (u b)").bitcast(BF16).rearrange("p (u b e) -> p u e b", u=2, e=2)
+            dst = wt[(g, m)][:].rearrange("p (b q) -> p q b", q=4)
+            nc.scalar.activation(out=dst[:, q, :], in_=src[:, q // 2, q % 2, :], func=ACT.Copy,
+                                 scale=maskT[:, g * M + m, q:q + 1])
 
         def quant_x(g, m, lo=0, hi=B):
             if g not in xc:
@@ -276,20 +281,22 @@ def tile_dynamicfeaturegroupinglayer_kernel(tc, x, W_masks, W1, W2, ln1_w, ln1_b
             else:
                 wfill_t(0, f, ph, "hz")
             wfill_copy(0, f, f >= 2)
-        nc.vector.tensor_scalar(out=mask_sb[0:GM, :], in0=e_sb[0:GM, :], scalar1=msc[0:GM, :], scalar2=None,
-                                op0=ALU.mult)
+        nc.vector.tensor_scalar(out=mask_sb[0:GM], in0=e_sb[0:GM, :].rearrange("r (p q) -> r q p", q=4),
+                                scalar1=msc[0:GM, :], scalar2=None, op0=ALU.mult)
         quant_w(0, 0)
-        quant_w(0, 1)
         for q in range(4):
-            nc.tensor.transpose(mps[:, q, :], mask_sb[:, q:S:4], ident[:])
+            nc.tensor.transpose(mps[:, q, :], mask_sb[:, q, :], ident[:])
         maskT = const.tile([P, GM, 4], F32, name="maskT")
         nc.vector.tensor_copy(out=maskT[:], in_=mps[:, :, 0:GM].rearrange("p t c -> p c t"))
+        quant_w(0, 1)
         weighted(0, 0, 0, P)
         x_t(1, pz, "zT")
         weighted(0, 1, 0, P)
         quant_x(0, 0, 0, P)
         mx(0, False)
         wfill_t(1, 0, pprep, "prep")
+        for i in range(3):
+            weighted_s(1, 3 + i // 4, i % 4)
         lnf = const.tile([P, 2, P], F32, name="lnf")
         lnT = const.tile([P, 2, P], F32, name="lnT")
 
@@ -315,7 +322,7 @@ def tile_dynamicfeaturegroupinglayer_kernel(tc, x, W_masks, W1, W2, ln1_w, ln1_b
                 weighted(0, 2, P, B)
                 weighted(0, 3, P, B)
                 quant_x(0, 0, P, B)
-            elif t < 7:
+            elif t < 6:
                 weighted(1, t - 3)
             if 5 <= t < 7:
                 quant_w(1, t - 5)
@@ -344,6 +351,8 @@ def tile_dynamicfeaturegroupinglayer_kernel(tc, x, W_masks, W1, W2, ln1_w, ln1_b
                     quant_w(g, 1)
 
         def prep_s(t):
+            for i in {0: (3,)}.get(t, ()):
+                weighted_s(1, 3 + i // 4, i % 4)
             if t < 4:
                 wfill_copy(1, t, True)
 

@@ -295,8 +295,8 @@ def tile_dynamicfeaturegroupinglayer_kernel(tc, x, W_masks, W1, W2, ln1_w, ln1_b
         quant_x(0, 0, 0, P)
         mx(0, False)
         wfill_t(1, 0, pprep, "prep")
-        for i in range(3):
-            weighted_s(1, 3 + i // 4, i % 4)
+        for i in range(4):
+            weighted_s(1, 2 + i // 4, i % 4)
         lnf = const.tile([P, 2, P], F32, name="lnf")
         lnT = const.tile([P, 2, P], F32, name="lnT")
 
@@ -322,7 +322,7 @@ def tile_dynamicfeaturegroupinglayer_kernel(tc, x, W_masks, W1, W2, ln1_w, ln1_b
                 weighted(0, 2, P, B)
                 weighted(0, 3, P, B)
                 quant_x(0, 0, P, B)
-            elif t < 6:
+            elif t < 5:
                 weighted(1, t - 3)
             if 5 <= t < 7:
                 quant_w(1, t - 5)
@@ -351,8 +351,8 @@ def tile_dynamicfeaturegroupinglayer_kernel(tc, x, W_masks, W1, W2, ln1_w, ln1_b
                     quant_w(g, 1)
 
         def prep_s(t):
-            for i in {0: (3,)}.get(t, ()):
-                weighted_s(1, 3 + i // 4, i % 4)
+            for i in {1: (4, 5), 2: (6, 7)}.get(t, ()):
+                weighted_s(1, 2 + i // 4, i % 4)
             if t < 4:
                 wfill_copy(1, t, True)
 
@@ -366,10 +366,10 @@ def tile_dynamicfeaturegroupinglayer_kernel(tc, x, W_masks, W1, W2, ln1_w, ln1_b
                 x_t(g, pprep, "prep")
             elif k >= 4:
                 wfill_t(g, k - 4, pprep, "prep")
-        for t in range(NSTEP + 9):
+        for t in range(NSTEP + 10):
             ta = t - 7
             tm = ta - 1
-            tf = t - 9
+            tf = t - 10
             zs = [(t - 3, True)] if 0 <= t - 3 < NSTEP else []
             zvec = 0 if t < V_TAKES_Z else 1
             own = t < NSTEP + 3 or t % 2 == 0
@@ -391,8 +391,6 @@ def tile_dynamicfeaturegroupinglayer_kernel(tc, x, W_masks, W1, W2, ln1_w, ln1_b
                 ag(t)
             if t + 1 < NSTEP:
                 mx(t + 1, False)
-            if t < NSTEP:
-                prep_pe(t)
             if 0 <= ta < NSTEP:
                 own = t < NSTEP + 3 or t % 2 == 0
                 tr(ta // 4, 2 * (ta % 4), own)
@@ -404,6 +402,8 @@ def tile_dynamicfeaturegroupinglayer_kernel(tc, x, W_masks, W1, W2, ln1_w, ln1_b
             if 0 <= ta < NSTEP:
                 act_sig(ta // 4, ta % 4)
                 act_relu(ta // 4, ta % 4, t > V_TAKES_RELU and t % 2 == 1)
+            if t < NSTEP:
+                prep_pe(t)
             if 0 <= tf < NSTEP:
                 acc(tf // 4, tf % 4)
             if 0 <= tf < NSTEP and tf % 4 == 3:

from contextlib import ExitStack

import concourse.mybir as mybir
from concourse.masks import make_identity

F32 = mybir.dt.float32
BF16 = mybir.dt.bfloat16
U32 = mybir.dt.uint32
U8 = mybir.dt.uint8
FP8X4 = mybir.dt.float8_e4m3fn_x4
ALU = mybir.AluOpType
ACT = mybir.ActivationFunctionType
AX = mybir.AxisListType

B, G, M, S, H = 256, 10, 4, 512, 512
ALPHA = 1.1
EPS = 1e-5
P = 128
FLOPS = 2 * 2 * B * G * M * S * H

NSTEP = G * 2 * M
GM = G * M
V_TAKES_Z = 8 * (G - 1)
V_TAKES_RELU = NSTEP
NST = 2


def tile_dynamicfeaturegroupinglayer_kernel(tc, x, W_masks, W1, W2, ln1_w, ln1_b, ln2_w, ln2_b, out):
    nc = tc.nc
    with ExitStack() as ctx:
        ctx.enter_context(tc.manual_schedule())
        const = ctx.enter_context(tc.tile_pool(name="const", bufs=1))
        wrawp = ctx.enter_context(tc.tile_pool(name="wrawp", bufs=3))
        prepp = ctx.enter_context(tc.tile_pool(name="prepp", bufs=2))
        qp = ctx.enter_context(tc.tile_pool(name="qp", bufs=3))
        wtp = ctx.enter_context(tc.tile_pool(name="wtp", bufs=8))
        small = ctx.enter_context(tc.tile_pool(name="small", bufs=5))
        zp = ctx.enter_context(tc.tile_pool(name="zp", bufs=2))
        ap3 = ctx.enter_context(tc.tile_pool(name="ap3", bufs=4))
        outp = ctx.enter_context(tc.tile_pool(name="outp", bufs=2))
        ps = ctx.enter_context(tc.psum_pool(name="ps", bufs=2))
        ph = ctx.enter_context(tc.psum_pool(name="ph", bufs=2))
        pz = ctx.enter_context(tc.psum_pool(name="pz", bufs=2))
        pprep = ctx.enter_context(tc.psum_pool(name="pprep", bufs=1))
        pfin = ctx.enter_context(tc.psum_pool(name="pfin", bufs=1))

        wm = const.tile([P, S], BF16, name="wm")
        nc.sync.dma_start(out=wm[0:GM, :], in_=W_masks.rearrange("g m s -> (g m) s"))
        x_sb = const.tile([P, 2, G * S], BF16, name="x_sb")
        for bh in range(2):
            nc.sync.dma_start(out=x_sb[:, bh, 0:S], in_=x[bh * P:(bh + 1) * P, 0:S])

        wraw = {}

        def load_w(g):
            t_ = wrawp.tile([P, 2, 4, S], BF16, name="wraw", tag="wraw")
            nc.sync.dma_start(out=t_[:, 0], in_=W1[g].rearrange("(t p) s -> p t s", p=P))
            nc.sync.dma_start(out=t_[:, 1], in_=W2[g].rearrange("(t p) s -> p t s", p=P))
            wraw[g] = t_

        load_w(0)
        for bh in range(2):
            nc.sync.dma_start(out=x_sb[:, bh, S:2 * S], in_=x[bh * P:(bh + 1) * P, S:2 * S])
        load_w(1)
        lnraw = const.tile([P, 2, P], BF16, name="lnraw")
        nc.vector.memset(lnraw[:], 0.0)
        nc.sync.dma_start(out=lnraw[0:GM, 0, :], in_=ln1_w.rearrange("g (t p) -> (g t) p", p=P))
        nc.sync.dma_start(out=lnraw[GM:2 * GM, 0, :], in_=ln1_b.rearrange("g (t p) -> (g t) p", p=P))
        nc.sync.dma_start(out=lnraw[0:GM, 1, :], in_=ln2_w.rearrange("g (t p) -> (g t) p", p=P))
        nc.sync.dma_start(out=lnraw[GM:2 * GM, 1, :], in_=ln2_b.rearrange("g (t p) -> (g t) p", p=P))
        for bh in range(2):
            nc.sync.dma_start(out=x_sb[:, bh, 2 * S:G * S], in_=x[bh * P:(bh + 1) * P, 2 * S:G * S])

        ident = const.tile([P, P], F32, name="ident")
        make_identity(nc, ident[:])
        one = const.tile([P, 1], F32, name="one")
        nc.vector.memset(one[:], 1.0)
        warm = const.tile([P, 1], F32, name="warm")
        nc.scalar.activation(out=warm[:], in_=one[:], func=ACT.Exp)
        cexp = const.tile([P, 4], F32, name="cexp")
        nc.vector.memset(cexp[:], -0.5)
        cneg = const.tile([P, 4], F32, name="cneg")
        nc.vector.memset(cneg[:], -1.0)
        cal = const.tile([P, 1], F32, name="cal")
        nc.vector.tensor_scalar(out=cal[:], in0=one[:], scalar1=-1.0 / ALPHA, scalar2=None, op0=ALU.mult)
        ones = const.tile([P, 4], F32, name="ones")
        nc.vector.memset(ones[:], 1.0)
        stt = []
        for i in range(NST):
            st = const.tile([P, 4, 9], F32, name="st%d" % i)
            nc.vector.memset(st[:], 0.0)
            nc.vector.tensor_scalar(out=st[:, :, 8], in0=ones[:], scalar1=H * EPS, scalar2=None, op0=ALU.mult)
            stt.append(st)
        mask_sb = const.tile([P, 4, P], F32, name="mask_sb")
        nc.vector.memset(mask_sb[:], 0.0)

        mx_ = const.tile([P, 1], F32, name="mx_")
        nc.vector.reduce_max(out=mx_[0:GM, :], in_=wm[0:GM, :], axis=AX.X)
        nmxa = const.tile([P, 1], F32, name="nmxa")
        nc.scalar.mul(out=nmxa[0:GM, :], in_=mx_[0:GM, :], mul=-ALPHA)
        nmx = const.tile([P, 1], F32, name="nmx")
        nc.scalar.mul(out=nmx[0:GM, :], in_=mx_[0:GM, :], mul=-1.0)
        ea_sb = const.tile([P, S], F32, name="ea_sb")
        sa = const.tile([P, 1], F32, name="sa")
        nc.scalar.activation(out=ea_sb[0:GM, :], in_=wm[0:GM, :], func=ACT.Exp, bias=nmxa[0:GM, :], scale=ALPHA,
                             accum_out=sa[0:GM, :])
        e_sb = const.tile([P, S], F32, name="e_sb")
        nc.scalar.activation(out=e_sb[0:GM, :], in_=wm[0:GM, :], func=ACT.Exp, bias=nmx[0:GM, :], scale=1.0)
        nc.scalar.activation(out=warm[:], in_=one[:], func=ACT.Sigmoid)
        sae = const.tile([P, 1], F32, name="sae")
        nc.vector.tensor_scalar(out=sae[0:GM, :], in0=sa[0:GM, :], scalar1=EPS, scalar2=None, op0=ALU.add)
        msc = const.tile([P, 1], F32, name="msc")
        nc.gpsimd.tensor_tensor(out=msc[0:GM, :], in0=sae[0:GM, :], in1=cal[0:GM, :], op=ALU.pow)

        gw, wc, ws, xc, xs, xbank, wt, fillb = {}, {}, {}, {}, {}, {}, {}, {}

        def wfill_t(g, f, pool, tag):
            w, jh = f // 2, f % 2
            bank = pool.tile([P, 2, 256], F32, name="wbank", tag=tag)
            for u in range(2):
                for jl in range(2):
                    src = wraw[g][:, w, 2 * jh + jl, :].bitcast(F32)
                    nc.tensor.transpose(bank[:, u, jl * P:(jl + 1) * P], src[:, u:256:2], ident[:])
            fillb[(g, f)] = bank

        def wfill_copy(g, f, on_scalar):
            w, jh = f // 2, f % 2
            if jh == 0:
                gw[(g, w)] = prepp.tile([P, 4 * H], BF16, name="gw", tag="gw", align_bytes=64)
            dst = gw[(g, w)][:].bitcast(F32).rearrange("p (j u) -> p j u", u=2)
            src = fillb[(g, f)][:].rearrange("p u j -> p j u")
            if on_scalar:
                nc.scalar.copy(out=dst[:, jh * 256:(jh + 1) * 256, :], in_=src)
            else:
                nc.vector.tensor_copy(out=dst[:, jh * 256:(jh + 1) * 256, :], in_=src)

        def quant_w(g, w):
            if w == 0:
                wc[g] = qp.tile([P, 2, H], U32, name="wc", tag="wc", align_bytes=64)
                ws[g] = qp.tile([P, 2, H], U8, name="ws", tag="ws", align_bytes=64)
            nc.vector.quantize_mx(out=wc[g][:, w, :].bitcast(FP8X4), scales=ws[g][:, w, :], in_=gw[(g, w)][:])

        def x_t(g, pool, tag):
            bank = pool.tile([P, 2, 256], F32, name="xbank", tag=tag)
            for u in range(2):
                for bh in range(2):
                    src = x_sb[:, bh, :].bitcast(F32)
                    nc.tensor.transpose(bank[:, u, bh * P:(bh + 1) * P],
                                        src[:, 256 * g + u:256 * (g + 1):2], ident[:])
            xbank[g] = bank

        def weighted(g, m, lo=0, hi=B):
            if lo == 0:
                wt[(g, m)] = wtp.tile([P, 4 * B], BF16, name="wt", tag="wt", align_bytes=64)
            in0 = xbank[g][:].rearrange("p u b -> p (u b)").bitcast(BF16).rearrange("p (u b e) -> p b u e", u=2, e=2)
            in1 = maskT[:, g * M + m, :].rearrange("p (u e) -> p u e", u=2).unsqueeze(1)
            nc.vector.tensor_tensor(out=wt[(g, m)][:, 4 * lo:4 * hi].rearrange("p (b u e) -> p b u e", u=2, e=2),
                                    in0=in0[:, lo:hi], in1=in1.to_broadcast([P, hi - lo, 2, 2]), op=ALU.mult)

        def weighted_s(g, m, q):
            if q == 0:
                wt[(g, m)] = wtp.tile([P, 4 * B], BF16, name="wt", tag="wt", align_bytes=64)
            src = xbank[g][:].rearrange("p u b -> p (u b)").bitcast(BF16).rearrange("p (u b e) -> p u e b", u=2, e=2)
            dst = wt[(g, m)][:].rearrange("p (b q) -> p q b", q=4)
            nc.scalar.activation(out=dst[:, q, :], in_=src[:, q // 2, q % 2, :], func=ACT.Copy,
                                 scale=maskT[:, g * M + m, q:q + 1])

        def quant_x(g, m, lo=0, hi=B):
            if g not in xc:
                xc[g] = qp.tile([P, M, B], U32, name="xc", tag="xc", align_bytes=64)
                xs[g] = qp.tile([P, M, B], U8, name="xs", tag="xs", align_bytes=64)
            nc.vector.quantize_mx(out=xc[g][:, m, lo:hi].bitcast(FP8X4), scales=xs[g][:, m, lo:hi],
                                  in_=wt[(g, m)][:, 4 * lo:4 * hi])

        mvt, nrt, nbt = {}, {}, {}
        hbank, zt, zbank, sig, r2, prod, finb = {}, {}, {}, {}, {}, {}, {}

        def mx(t, for_z):
            g, bh, m = t // 8, (t % 8) // 4, t % 4
            cols = slice(bh * P, (bh + 1) * P)
            for w in range(2):
                if for_z:
                    bank = ph.tile([P, H], F32, name="hz", tag="hz")
                else:
                    bank = ps.tile([P, H], F32, name="hs", tag="hs")
                hbank[(t, w)] = bank
                nc.tensor.matmul_mx(out=bank[:], lhsT=xc[g][:, m, cols].bitcast(FP8X4), lhsT_scale=xs[g][:, m, cols],
                                    rhs=wc[g][:, w, :].bitcast(FP8X4), rhs_scale=ws[g][:, w, :],
                                    start=True, stop=True)

        def bn(t):
            for w in range(2):
                nc.vector.bn_stats(out=stt[(t // 2) % NST][:, 2 * (t % 2) + w, 0:6], in_=hbank[(t, w)][:])

        def ag(t):
            ss = t // 2
            if ss not in mvt:
                mvt[ss] = small.tile([P, 4, 2], F32, name="mv", tag="mv")
            for w in range(2):
                i = 2 * (t % 2) + w
                nc.vector.bn_aggr(out=mvt[ss][:, i, :], in_=stt[ss % NST][:, i, :])

        def chain(ss):
            rs = small.tile([P, 4], F32, name="rs", tag="rs")
            nc.gpsimd.tensor_tensor(out=rs[:], in0=mvt[ss][:, :, 1], in1=cexp[:], op=ALU.pow)
            nrt[ss] = small.tile([P, 4], F32, name="nr", tag="nr")
            nc.gpsimd.tensor_tensor(out=nrt[ss][:], in0=rs[:], in1=cneg[:], op=ALU.mult)
            nbt[ss] = small.tile([P, 4], F32, name="nb", tag="nb")
            nc.gpsimd.tensor_tensor(out=nbt[ss][:], in0=mvt[ss][:, :, 0], in1=rs[:], op=ALU.mult)

        def z_dst(t, w):
            ss, m = t // 4, t % 4
            if ss not in zt:
                zt[ss] = zp.tile([P, 2, M, H], F32, name="z", tag="z")
            return zt[ss][:, w, m, :]

        def z_scalar(t, w):
            ss, i = t // 2, 2 * (t % 2) + w
            nc.scalar.activation(out=z_dst(t, w), in_=hbank[(t, w)][:], func=ACT.Identity,
                                 bias=nbt[ss][:, i:i + 1], scale=nrt[ss][:, i:i + 1])

        def z_vector(t, w):
            ss, i = t // 2, 2 * (t % 2) + w
            nc.vector.tensor_scalar(out=z_dst(t, w), in0=hbank[(t, w)][:], scalar1=mvt[ss][:, i, 0:1],
                                    scalar2=nrt[ss][:, i:i + 1], op0=ALU.subtract, op1=ALU.mult)

        def tr(ss, k, own):
            jt, w = k // 2, k % 2
            if own:
                bank = pz.tile([P, M, P], F32, name="zT", tag="zT")
            else:
                bank = ph.tile([P, M, P], F32, name="zTh", tag="hz")
            for m in range(M):
                nc.tensor.transpose(bank[:, m, :], zt[ss][:, w, m, jt * P:(jt + 1) * P], ident[:])
            zbank[(ss, k)] = bank

        def act_sig(ss, jt):
            c = (ss // 2) * 4 + jt
            sig[(ss, jt)] = ap3.tile([P, M * P], F32, name="sig", tag="sig")
            nc.scalar.activation(out=sig[(ss, jt)][:], in_=zbank[(ss, 2 * jt)][:].rearrange("p m b -> p (m b)"),
                                 func=ACT.Sigmoid, bias=lnT[:, 0, GM + c:GM + c + 1], scale=lnT[:, 0, c:c + 1])

        def act_relu(ss, jt, on_vector):
            c = (ss // 2) * 4 + jt
            r2[(ss, jt)] = ap3.tile([P, M * P], F32, name="r2", tag="r2")
            src = zbank[(ss, 2 * jt + 1)][:].rearrange("p m b -> p (m b)")
            if on_vector:
                nc.vector.tensor_scalar(out=r2[(ss, jt)][:], in0=src, scalar1=lnT[:, 1, c:c + 1],
                                        scalar2=lnT[:, 1, GM + c:GM + c + 1], op0=ALU.mult, op1=ALU.add)
            else:
                nc.scalar.activation(out=r2[(ss, jt)][:], in_=src, func=ACT.Relu,
                                     bias=lnT[:, 1, GM + c:GM + c + 1], scale=lnT[:, 1, c:c + 1])

        def mul(ss, jt, on_vector):
            prod[(ss, jt)] = ap3.tile([P, M, P], F32, name="prod", tag="prod")
            dst = prod[(ss, jt)][:].rearrange("p m b -> p (m b)")
            if on_vector:
                nc.vector.scalar_tensor_tensor(out=dst, in0=r2[(ss, jt)][:], scalar=0.0, in1=sig[(ss, jt)][:],
                                               op0=ALU.max, op1=ALU.mult)
            else:
                nc.gpsimd.tensor_tensor(out=dst, in0=sig[(ss, jt)][:], in1=r2[(ss, jt)][:], op=ALU.mult)

        def acc(ss, jt):
            if jt == 0:
                finb[ss] = pfin.tile([P, H], F32, name="fin", tag="fin")
            for m in range(M):
                nc.tensor.matmul(finb[ss][:, jt * P:(jt + 1) * P], lhsT=prod[(ss, jt)][:, m, :], rhs=ident[:],
                                 is_transpose=True, start=(m == 0), stop=(m == M - 1))

        def fin(ss):
            g, bh = ss // 2, ss % 2
            ot = outp.tile([P, H], F32, name="ot", tag="ot")
            nc.scalar.copy(out=ot[:], in_=finb[ss][:])
            nc.sync.dma_start(out=out[bh * P:(bh + 1) * P, g * H:(g + 1) * H], in_=ot[:])

        mps = pz.tile([P, 4, P], F32, name="mps", tag="zT")
        x_t(0, pz, "zT")
        for f in range(4):
            if f < 2:
                wfill_t(0, f, ps, "hs")
            else:
                wfill_t(0, f, ph, "hz")
            wfill_copy(0, f, f >= 2)
        nc.vector.tensor_scalar(out=mask_sb[0:GM], in0=e_sb[0:GM, :].rearrange("r (p q) -> r q p", q=4),
                                scalar1=msc[0:GM, :], scalar2=None, op0=ALU.mult)
        quant_w(0, 0)
        for q in range(4):
            nc.tensor.transpose(mps[:, q, :], mask_sb[:, q, :], ident[:])
        maskT = const.tile([P, GM, 4], F32, name="maskT")
        nc.vector.tensor_copy(out=maskT[:], in_=mps[:, :, 0:GM].rearrange("p t c -> p c t"))
        quant_w(0, 1)
        weighted(0, 0, 0, P)
        x_t(1, pz, "zT")
        weighted(0, 1, 0, P)
        quant_x(0, 0, 0, P)
        mx(0, False)
        wfill_t(1, 0, pprep, "prep")
        for i in range(4):
            weighted_s(1, 2 + i // 4, i % 4)
        lnf = const.tile([P, 2, P], F32, name="lnf")
        lnT = const.tile([P, 2, P], F32, name="lnT")

        def ln_in():
            nc.vector.tensor_copy(out=lnf[:], in_=lnraw[:])

        def ln_t():
            lps = pfin.tile([P, 2, P], F32, name="lps", tag="fin")
            for a in range(2):
                nc.tensor.transpose(lps[:, a, :], lnf[:, a, :], ident[:])
            nc.vector.tensor_scalar(out=lnT[:, :, 0:GM], in0=lps[:, :, 0:GM], scalar1=-1.0, scalar2=None, op0=ALU.mult)
            nc.vector.tensor_copy(out=lnT[:, :, GM:2 * GM], in_=lps[:, :, GM:2 * GM])

        def prep_v(t):
            if t < 3:
                quant_x(0, t + 1, 0, P)
            elif t < 6:
                quant_x(0, t - 2, P, B)
            if t < 2:
                weighted(0, t + 2, 0, P)
                weighted(0, t, P, B)
            elif t == 2:
                weighted(0, 2, P, B)
                weighted(0, 3, P, B)
                quant_x(0, 0, P, B)
            elif t < 5:
                weighted(1, t - 3)
            if 5 <= t < 7:
                quant_w(1, t - 5)
            if 5 <= t < 9:
                quant_x(1, t - 5)
            if t == 4:
                ln_in()
            elif t == 5:
                ln_t()
            g, k = (t + 1) // 8 + 1, (t + 1) % 8
            if g < 2 or g >= G:
                return
            if k < 4:
                weighted(g, k)
            else:
                wfill_copy(g, k - 4, False)
                if k == 4:
                    quant_x(g, 0)
                    quant_x(g, 1)
                elif k == 5:
                    quant_x(g, 2)
                elif k == 6:
                    quant_w(g, 0)
                else:
                    quant_x(g, 3)
                    quant_w(g, 1)

        def prep_s(t):
            for i in {1: (4, 5), 2: (6, 7)}.get(t, ()):
                weighted_s(1, 2 + i // 4, i % 4)
            if t < 4:
                wfill_copy(1, t, True)

        def prep_pe(t):
            if t < 3:
                wfill_t(1, t + 1, pprep, "prep")
            g, k = (t + 2) // 8 + 1, (t + 2) % 8
            if g < 2 or g >= G:
                return
            if k == 0:
                x_t(g, pprep, "prep")
            elif k >= 4:
                wfill_t(g, k - 4, pprep, "prep")
        for t in range(NSTEP + 10):
            ta = t - 7
            tm = ta - 1
            tf = t - 10
            zs = [(t - 3, True)] if 0 <= t - 3 < NSTEP else []
            zvec = 0 if t < V_TAKES_Z else 1
            own = t < NSTEP + 3 or t % 2 == 0
            if t % 8 == 0 and t // 8 + 2 < G:
                load_w(t // 8 + 2)
            for i, b in zs:
                mx(i, b)
            if t < NSTEP:
                bn(t)
            if t < NSTEP:
                prep_v(t)
            for i, b in zs:
                for w in range(2):
                    if w < 2 - zvec:
                        z_scalar(i, w)
                    else:
                        z_vector(i, w)
            if t < NSTEP:
                ag(t)
            if t + 1 < NSTEP:
                mx(t + 1, False)
            if 0 <= ta < NSTEP:
                own = t < NSTEP + 3 or t % 2 == 0
                tr(ta // 4, 2 * (ta % 4), own)
                tr(ta // 4, 2 * (ta % 4) + 1, own)
            if 0 <= tm < NSTEP:
                mul(tm // 4, tm % 4, t >= V_TAKES_RELU)
            if t < NSTEP and t % 2 == 1:
                chain(t // 2)
            if 0 <= ta < NSTEP:
                act_sig(ta // 4, ta % 4)
                act_relu(ta // 4, ta % 4, t > V_TAKES_RELU and t % 2 == 1)
            if t < NSTEP:
                prep_pe(t)
            if 0 <= tf < NSTEP:
                acc(tf // 4, tf % 4)
            if 0 <= tf < NSTEP and tf % 4 == 3:
                fin(tf // 4)
            prep_s(t)
